import numpy as np
import ml_dtypes


def mxq(x, axis, fmt="e4m3"):
    dtype, down = {"e4m3": (ml_dtypes.float8_e4m3fn, 7), "e5m2": (ml_dtypes.float8_e5m2, 14)}[fmt]
    v = np.moveaxis(np.asarray(x, np.float32).astype(ml_dtypes.bfloat16).astype(np.float64), axis, -1)
    blocks = v.reshape(v.shape[:-1] + (-1, 32))
    amax = np.abs(blocks).max(-1, keepdims=True)
    byte = np.maximum(np.where(amax > 0, np.frexp(amax)[1] - 1 + 127, 0) - down, 1)
    scale = np.exp2(byte - 127.0)
    codes = (blocks / scale).astype(np.float32).astype(dtype).astype(np.float64)
    return np.moveaxis((codes * scale).reshape(v.shape), -1, axis)


WIDE = False


def mx_kscale(k):
    if not WIDE:
        return np.ones(k)
    levels = np.array([10, -10, 5, -5, 0])
    a = np.random.permutation(np.resize(levels, k // 512 * 4)).reshape(k // 512, 4)
    idx = np.arange(k)
    return np.exp2(a[idx // 512, idx % 128 // 32])


BF16 = ml_dtypes.bfloat16


def bf(x):
    return np.asarray(x, np.float32).astype(BF16)


def f64(x):
    return np.asarray(x).astype(np.float64)


B, N, D = 4, 512, 1024


def row_normalize(adj):
    rowsum = adj.sum(axis=-1, keepdims=True)
    r_inv = np.where(rowsum == 0, 0.0, 1.0 / np.where(rowsum == 0, 1.0, rowsum))
    return adj * r_inv


def setup_inputs():
    s = mx_kscale(D)
    return {"X": bf(np.random.standard_normal((B, N, D)) * s),
            "adj": bf(np.random.uniform(0.0, 1.0, (B, N, N))),
            "W_l": bf(np.random.uniform(-1.0, 1.0, (D, D)) / np.sqrt(D) / s[:, None]),
            "W_l1": bf(np.random.uniform(-1.0, 1.0, (D, D)) * 0.3 * np.sqrt(N) / np.sqrt(D) / s[:, None])}


def reference(X, adj, W_l, W_l1):
    adj_n = row_normalize(f64(adj))
    Xq = mxq(f64(X), 2, "e4m3")
    e1 = Xq @ mxq(f64(W_l1), 0, "e4m3")
    e11 = mxq(adj_n, 2, "e4m3") @ mxq(e1, 1, "e4m3")
    X1 = Xq @ mxq(f64(W_l), 0, "e4m3")
    h = X1 + e11
    return np.where(h >= 0, h, 0.01 * h)

@@ -1,0 +1,289 @@
+from contextlib import ExitStack
+
+import concourse.mybir as mybir
+from concourse.masks import make_identity
+
+F32 = mybir.dt.float32
+BF16 = mybir.dt.bfloat16
+U32 = mybir.dt.uint32
+U8 = mybir.dt.uint8
+FP8X4 = mybir.dt.float8_e4m3fn_x4
+ALU = mybir.AluOpType
+AX = mybir.AxisListType
+
+P = 128
+B = 4
+N = 512
+D = 1024
+NT = N // P
+G = D // 512
+
+FLOPS = 2 * (B * N) * D * D * 2 + 2 * B * N * N * D
+
+MANUAL = True
+
+
+def tile_graphnet_kernel(tc, X, adj, W_l, W_l1, out):
+    nc = tc.nc
+    with ExitStack() as ctx:
+        if MANUAL:
+            ctx.enter_context(tc.manual_schedule())
+        keep = ctx.enter_context(tc.tile_pool(name="keep", bufs=1))
+        stage = ctx.enter_context(tc.tile_pool(name="stage", bufs=2))
+        psum = ctx.enter_context(tc.psum_pool(name="psum", bufs=8))
+
+        ident_f = keep.tile([P, P], F32, name="ident_f")
+        make_identity(nc, ident_f[:])
+        ident_b = keep.tile([P, P], BF16, name="ident_b")
+        make_identity(nc, ident_b[:])
+
+        x_raw = [keep.tile([P, NT * D], BF16, name="x_raw%d" % b, tag="x_raw", bufs=3) for b in range(B)]
+        a_raw = [keep.tile([P, NT, N], BF16, name="a_raw%d" % b) for b in range(B)]
+        w_raw = [keep.tile([P, G, 4, D], BF16, name="w_raw%d" % i) for i in range(2)]
+        x_cod = [keep.tile([P, G * N], U32, name="x_cod%d" % b, align_bytes=64) for b in range(B)]
+        x_scl = [keep.tile([P, G * N], U8, name="x_scl%d" % b, align_bytes=64) for b in range(B)]
+        w_cod = [keep.tile([P, G * D], U32, name="w_cod%d" % i, align_bytes=64) for i in range(2)]
+        w_scl = [keep.tile([P, G * D], U8, name="w_scl%d" % i, align_bytes=64) for i in range(2)]
+        a_cod = [keep.tile([P, N], U32, name="a_cod%d" % b, align_bytes=64) for b in range(B)]
+        a_scl = [keep.tile([P, N], U8, name="a_scl%d" % b, align_bytes=64) for b in range(B)]
+        e_cod = [keep.tile([P, D], U32, name="e_cod%d" % b, tag="e_cod", bufs=3, align_bytes=64) for b in range(B)]
+        e_scl = [keep.tile([P, D], U8, name="e_scl%d" % b, tag="e_scl", bufs=3, align_bytes=64) for b in range(B)]
+
+        def load_x(b):
+            nc.sync.dma_start(
+                out=x_raw[b][:].rearrange("p (t d) -> p t d", t=NT),
+                in_=X[b].rearrange("(t p) d -> p t d", p=P),
+            )
+
+        def load_a(b):
+            nc.sync.dma_start(out=a_raw[b][:], in_=adj[b].rearrange("(t p) j -> p t j", p=P))
+
+        def load_w_cols(i, W, h, e):
+            dst = w_raw[i][:].rearrange("p g (u e) n -> p (g u) e n", e=2)
+            src = W.rearrange("(q p e) n -> p q e n", q=4, p=P, e=2)
+            nc.sync.dma_start(
+                out=dst[:, :, e, 512 * h : 512 * h + 512], in_=src[:, :, e, 512 * h : 512 * h + 512]
+            )
+
+        def load_w_pass(i, W, g):
+            dst = w_raw[i][:, g].rearrange("p (u e) n -> p u e n", e=2)
+            src = W[512 * g : 512 * g + 512, :].rearrange("(u p e) n -> p u e n", u=2, p=P, e=2)
+            nc.sync.dma_start(out=dst, in_=src)
+
+        load_x(0)
+        for h in range(2):
+            for e in range(2):
+                load_w_cols(1, W_l1, h, e)
+        load_x(1)
+        load_a(0)
+        for g in range(G):
+            load_w_pass(0, W_l, g)
+        load_x(2)
+        load_a(1)
+        load_x(3)
+        load_a(2)
+        load_a(3)
+
+        def evac(eng, dst, src):
+            if eng == "S":
+                nc.scalar.copy(out=dst, in_=src)
+            else:
+                nc.vector.tensor_copy(out=dst, in_=src)
+
+        xg = {}
+
+        def transpose_x(b, engs):
+            xg[b] = stage.tile([P, G * N * 4], BF16, name="xg%d" % b, tag="xg", align_bytes=64)
+            xw = x_raw[b][:].bitcast(F32)
+            dst = xg[b][:].bitcast(F32).rearrange("p (g n u) -> p g n u", g=G, u=2)
+            c = 0
+            for g in range(G):
+                for hn in range(2):
+                    bank = psum.tile([P, 2, 256], F32, name="bx", tag="bank")
+                    for u in range(2):
+                        for tt in range(2):
+                            col = 512 * (2 * hn + tt) + 256 * g + 128 * u
+                            nc.tensor.transpose(
+                                bank[:, u, 128 * tt : 128 * tt + 128], xw[:, col : col + 128], ident_f[:]
+                            )
+                    evac(engs[c], dst[:, g, 256 * hn : 256 * hn + 256, :], bank[:].rearrange("p u n -> p n u"))
+                    c += 1
+
+        def quant_x(b):
+            nc.vector.quantize_mx(out=x_cod[b][:].bitcast(FP8X4), scales=x_scl[b][:], in_=xg[b][:])
+
+        wg = {}
+
+        def regroup_w(i, g, h, eng):
+            t = stage.tile([P, 512, 4], BF16, name="wg", tag="wg", bufs=4, align_bytes=64)
+            wg[(i, g, h)] = t
+            src = w_raw[i][:, g, :, 512 * h : 512 * h + 512]
+            evac(
+                eng,
+                t[:].rearrange("p (c i) t -> p c t i", i=4),
+                src.rearrange("p t (c i) -> p c t i", i=4),
+            )
+
+        def quant_w(i, g, h):
+            lo = D * g + 512 * h
+            nc.vector.quantize_mx(
+                out=w_cod[i][:, lo : lo + 512].bitcast(FP8X4),
+                scales=w_scl[i][:, lo : lo + 512],
+                in_=wg[(i, g, h)][:].rearrange("p c t -> p (c t)"),
+            )
+
+        eg = {}
+
+        def e1_blocks(b, wbs, engs):
+            if b not in eg:
+                eg[b] = stage.tile([P, D, 4], BF16, name="eg%d" % b, tag="eg", align_bytes=64)
+            for c, wb in enumerate(wbs):
+                bank = psum.tile([P, NT, P], F32, name="be", tag="bank")
+                for t in range(NT):
+                    for g in range(G):
+                        xl = N * g + P * t
+                        wl = D * g + P * wb
+                        nc.tensor.matmul_mx(
+                            out=bank[:, t, :],
+                            lhsT=x_cod[b][:, xl : xl + P].bitcast(FP8X4),
+                            lhsT_scale=x_scl[b][:, xl : xl + P],
+                            rhs=w_cod[1][:, wl : wl + P].bitcast(FP8X4),
+                            rhs_scale=w_scl[1][:, wl : wl + P],
+                            start=(g == 0),
+                            stop=(g == G - 1),
+                        )
+                evac(engs[c], eg[b][:, P * wb : P * wb + P, :], bank[:].rearrange("p t w -> p w t"))
+
+        def quant_e(b, h):
+            nc.vector.quantize_mx(
+                out=e_cod[b][:, 512 * h : 512 * h + 512].bitcast(FP8X4),
+                scales=e_scl[b][:, 512 * h : 512 * h + 512],
+                in_=eg[b][:, 512 * h : 512 * h + 512, :].rearrange("p c t -> p (c t)"),
+            )
+
+        an = {}
+
+        def adj_prep(b):
+            rs = stage.tile([P, NT], F32, name="rs", tag="rs")
+            nc.vector.tensor_reduce(out=rs[:], in_=a_raw[b][:], axis=AX.X, op=ALU.add)
+            zm = stage.tile([P, NT], F32, name="zm", tag="zm")
+            nc.vector.tensor_scalar(out=zm[:], in0=rs[:], scalar1=0.0, scalar2=None, op0=ALU.is_equal)
+            sf = stage.tile([P, NT], F32, name="sf", tag="sf")
+            nc.vector.tensor_tensor(out=sf[:], in0=rs[:], in1=zm[:], op=ALU.add)
+            rc = stage.tile([P, NT], F32, name="rc", tag="rc")
+            nc.vector.reciprocal(out=rc[:], in_=sf[:])
+            rr = stage.tile([P, NT], F32, name="rr", tag="rr")
+            nc.vector.tensor_tensor(out=rr[:], in0=rc[:], in1=zm[:], op=ALU.subtract)
+            an[b] = stage.tile([P, NT, N], BF16, name="an%d" % b, tag="an")
+            for t in range(NT):
+                nc.vector.tensor_scalar(
+                    out=an[b][:, t, :], in0=a_raw[b][:, t, :], scalar1=rr[:, t : t + 1], scalar2=None, op0=ALU.mult
+                )
+
+        ag = {}
+
+        def transpose_a(b, engs):
+            ag[b] = stage.tile([P, N, 4], BF16, name="ag%d" % b, tag="ag", align_bytes=64)
+            for hi in range(2):
+                bank = psum.tile([P, NT, 256], BF16, name="ba", tag="bank")
+                for tj in range(NT):
+                    for ii in range(2):
+                        nc.tensor.transpose(
+                            bank[:, tj, 128 * ii : 128 * ii + 128],
+                            an[b][:, 2 * hi + ii, 128 * tj : 128 * tj + 128],
+                            ident_b[:],
+                        )
+                evac(engs[hi], ag[b][:, 256 * hi : 256 * hi + 256, :], bank[:].rearrange("p t i -> p i t"))
+
+        def quant_a(b):
+            nc.vector.quantize_mx(
+                out=a_cod[b][:].bitcast(FP8X4), scales=a_scl[b][:], in_=ag[b][:].rearrange("p c t -> p (c t)")
+            )
+
+        def out_tiles(b, tis):
+            for ti in tis:
+                res = stage.tile([P, D], F32, name="res", tag="res", bufs=6)
+                for h in range(2):
+                    bank = psum.tile([P, 512], F32, name="bo", tag="bank")
+                    for g in range(G):
+                        xl = N * g + P * ti
+                        wl = D * g + 512 * h
+                        nc.tensor.matmul_mx(
+                            out=bank[:],
+                            lhsT=x_cod[b][:, xl : xl + P].bitcast(FP8X4),
+                            lhsT_scale=x_scl[b][:, xl : xl + P],
+                            rhs=w_cod[0][:, wl : wl + 512].bitcast(FP8X4),
+                            rhs_scale=w_scl[0][:, wl : wl + 512],
+                            start=(g == 0),
+                            stop=False,
+                        )
+                    nc.tensor.matmul_mx(
+                        out=bank[:],
+                        lhsT=a_cod[b][:, P * ti : P * ti + P].bitcast(FP8X4),
+                        lhsT_scale=a_scl[b][:, P * ti : P * ti + P],
+                        rhs=e_cod[b][:, 512 * h : 512 * h + 512].bitcast(FP8X4),
+                        rhs_scale=e_scl[b][:, 512 * h : 512 * h + 512],
+                        start=False,
+                        stop=True,
+                    )
+                    nc.scalar.copy(out=res[:, 512 * h : 512 * h + 512], in_=bank[:])
+                nc.vector.scalar_tensor_tensor(
+                    out=res[:], in0=res[:], scalar=0.01, in1=res[:], op0=ALU.mult, op1=ALU.max
+                )
+                nc.sync.dma_start(out=out[b, P * ti : P * ti + P, :], in_=res[:])
+
+        transpose_x(0, "SSSS")
+        regroup_w(1, 0, 0, "V")
+        regroup_w(1, 1, 0, "S")
+        quant_x(0)
+        quant_w(1, 0, 0)
+        quant_w(1, 1, 0)
+        regroup_w(1, 0, 1, "V")
+        regroup_w(1, 1, 1, "S")
+        e1_blocks(0, [0, 1, 2, 3], "SSSS")
+        quant_w(1, 0, 1)
+        quant_w(1, 1, 1)
+        transpose_x(1, "SSSS")
+        adj_prep(0)
+        e1_blocks(0, [4, 5, 6, 7], "SSSS")
+        quant_x(1)
+        quant_e(0, 0)
+        regroup_w(0, 0, 0, "V")
+        regroup_w(0, 1, 0, "V")
+        quant_e(0, 1)
+        quant_w(0, 0, 0)
+        quant_w(0, 1, 0)
+        e1_blocks(1, [0, 1, 2, 3, 4, 5, 6, 7], "SSSSSSSS")
+        regroup_w(0, 0, 1, "V")
+        regroup_w(0, 1, 1, "V")
+        quant_w(0, 0, 1)
+        quant_w(0, 1, 1)
+        transpose_a(0, "SS")
+        transpose_x(2, "SSSS")
+        quant_e(1, 0)
+        quant_a(0)
+        quant_e(1, 1)
+        quant_x(2)
+        out_tiles(0, [0, 1])
+        adj_prep(1)
+        out_tiles(0, [2, 3])
+        e1_blocks(2, [0, 1, 2, 3, 4, 5, 6, 7], "SSSSSSSS")
+        transpose_a(1, "SS")
+        transpose_x(3, "SSSS")
+        quant_e(2, 0)
+        quant_a(1)
+        quant_e(2, 1)
+        quant_x(3)
+        out_tiles(1, [0, 1])
+        adj_prep(2)
+        out_tiles(1, [2, 3])
+        e1_blocks(3, [0, 1, 2, 3, 4, 5, 6, 7], "SSSSSSSS")
+        adj_prep(3)
+        transpose_a(2, "SS")
+        transpose_a(3, "SS")
+        quant_e(3, 0)
+        quant_a(2)
+        quant_e(3, 1)
+        quant_a(3)
+        out_tiles(2, [0, 1, 2, 3])
+        out_tiles(3, [0, 1, 2, 3])

@@ -21,6 +21,84 @@ G = D // 512
 FLOPS = 2 * (B * N) * D * D * 2 + 2 * B * N * N * D
 
 MANUAL = True
+RES_BUFS = 6
+RS_ACC = True
+
+PLAN = [
+    ("LX",0),
+    ("LWC",1,0,0),
+    ("LWC",1,0,1),
+    ("LWC",1,1,0),
+    ("LWC",1,1,1),
+    ("LX",1),
+    ("LA",0),
+    ("LWP",0,0),
+    ("LWP",0,1),
+    ("LX",2),
+    ("LA",1),
+    ("LX",3),
+    ("LA",2),
+    ("LA",3),
+    ("TX",0,"SSSS"),
+    ("RW",1,0,0,"V"),
+    ("RW",1,1,0,"S"),
+    ("QX",0),
+    ("QW",1,0,0),
+    ("QW",1,1,0),
+    ("RW",1,0,1,"V"),
+    ("RW",1,1,1,"S"),
+    ("E",0,[0,1,2,3],"SSSS"),
+    ("QW",1,0,1),
+    ("QW",1,1,1),
+    ("TX",1,"SSSS"),
+    ("RS",0),
+    ("SCG",0),
+    ("E",0,[4,5,6,7],"SSSS"),
+    ("QX",1),
+    ("QE",0,0),
+    ("RW",0,0,0,"V"),
+    ("RW",0,1,0,"V"),
+    ("QE",0,1),
+    ("QW",0,0,0),
+    ("QW",0,1,0),
+    ("E",1,[0,1,2,3,4,5,6,7],"SSSSSSSS"),
+    ("RWG",0,0,1),
+    ("RWG",0,1,1),
+    ("QW",0,0,1),
+    ("QW",0,1,1),
+    ("TA",0,"SS"),
+    ("TX",2,"SSSS"),
+    ("QE",1,0),
+    ("QA",0),
+    ("QE",1,1),
+    ("QX",2),
+    ("O",0,[0,1]),
+    ("RS",1),
+    ("SCG",1),
+    ("O",0,[2,3]),
+    ("E",2,[0,1,2,3,4,5,6,7],"SSSSSSSS"),
+    ("TA",1,"SS"),
+    ("TX",3,"SSSS"),
+    ("QE",2,0),
+    ("QA",1),
+    ("QE",2,1),
+    ("QX",3),
+    ("O",1,[0,1]),
+    ("RS",2),
+    ("SCG",2),
+    ("O",1,[2,3]),
+    ("E",3,[0,1,2,3,4,5,6,7],"SSSSSSSS"),
+    ("RS",3),
+    ("SCG",3),
+    ("TA",2,"SS"),
+    ("TA",3,"SS"),
+    ("QE",3,0),
+    ("QA",2),
+    ("QE",3,1),
+    ("QA",3),
+    ("O",2,[0,1,2,3]),
+    ("O",3,[0,1,2,3]),
+]
 
 
 def tile_graphnet_kernel(tc, X, adj, W_l, W_l1, out):
@@ -48,41 +126,29 @@ def tile_graphnet_kernel(tc, X, adj, W_l, W_l1, out):
         a_scl = [keep.tile([P, N], U8, name="a_scl%d" % b, align_bytes=64) for b in range(B)]
         e_cod = [keep.tile([P, D], U32, name="e_cod%d" % b, tag="e_cod", bufs=3, align_bytes=64) for b in range(B)]
         e_scl = [keep.tile([P, D], U8, name="e_scl%d" % b, tag="e_scl", bufs=3, align_bytes=64) for b in range(B)]
+        W = [W_l, W_l1]
 
-        def load_x(b):
-            nc.sync.dma_start(
-                out=x_raw[b][:].rearrange("p (t d) -> p t d", t=NT),
-                in_=X[b].rearrange("(t p) d -> p t d", p=P),
-            )
+        def LX(b, parts=1):
+            dst = x_raw[b][:].rearrange("p (t d) -> p t d", t=NT)
+            src = X[b].rearrange("(t p) d -> p t d", p=P)
+            n = NT // parts
+            for k in range(parts):
+                nc.sync.dma_start(out=dst[:, n * k : n * k + n, :], in_=src[:, n * k : n * k + n, :])
 
-        def load_a(b):
+        def LA(b):
             nc.sync.dma_start(out=a_raw[b][:], in_=adj[b].rearrange("(t p) j -> p t j", p=P))
 
-        def load_w_cols(i, W, h, e):
+        def LWC(i, h, e):
             dst = w_raw[i][:].rearrange("p g (u e) n -> p (g u) e n", e=2)
-            src = W.rearrange("(q p e) n -> p q e n", q=4, p=P, e=2)
+            src = W[i].rearrange("(q p e) n -> p q e n", q=4, p=P, e=2)
             nc.sync.dma_start(
                 out=dst[:, :, e, 512 * h : 512 * h + 512], in_=src[:, :, e, 512 * h : 512 * h + 512]
             )
 
-        def load_w_pass(i, W, g):
+        def LWP(i, g):
             dst = w_raw[i][:, g].rearrange("p (u e) n -> p u e n", e=2)
-            src = W[512 * g : 512 * g + 512, :].rearrange("(u p e) n -> p u e n", u=2, p=P, e=2)
+            src = W[i][512 * g : 512 * g + 512, :].rearrange("(u p e) n -> p u e n", u=2, p=P, e=2)
             nc.sync.dma_start(out=dst, in_=src)
-
-        load_x(0)
-        for h in range(2):
-            for e in range(2):
-                load_w_cols(1, W_l1, h, e)
-        load_x(1)
-        load_a(0)
-        for g in range(G):
-            load_w_pass(0, W_l, g)
-        load_x(2)
-        load_a(1)
-        load_x(3)
-        load_a(2)
-        load_a(3)
 
         def evac(eng, dst, src):
             if eng == "S":
@@ -92,13 +158,13 @@ def tile_graphnet_kernel(tc, X, adj, W_l, W_l1, out):
 
         xg = {}
 
-        def transpose_x(b, engs):
+        def TX(b, engs):
             xg[b] = stage.tile([P, G * N * 4], BF16, name="xg%d" % b, tag="xg", align_bytes=64)
             xw = x_raw[b][:].bitcast(F32)
             dst = xg[b][:].bitcast(F32).rearrange("p (g n u) -> p g n u", g=G, u=2)
             c = 0
-            for g in range(G):
-                for hn in range(2):
+            for hn in range(2):
+                for g in range(G):
                     bank = psum.tile([P, 2, 256], F32, name="bx", tag="bank")
                     for u in range(2):
                         for tt in range(2):
@@ -109,22 +175,27 @@ def tile_graphnet_kernel(tc, X, adj, W_l, W_l1, out):
                     evac(engs[c], dst[:, g, 256 * hn : 256 * hn + 256, :], bank[:].rearrange("p u n -> p n u"))
                     c += 1
 
-        def quant_x(b):
+        def QX(b):
             nc.vector.quantize_mx(out=x_cod[b][:].bitcast(FP8X4), scales=x_scl[b][:], in_=xg[b][:])
 
         wg = {}
 
-        def regroup_w(i, g, h, eng):
+        def regroup(eng, t, i, g, lo, n):
+            src = w_raw[i][:, g, :, lo : lo + n]
+            evac(eng, t.rearrange("p (c i) t -> p c t i", i=4), src.rearrange("p t (c i) -> p c t i", i=4))
+
+        def RW(i, g, h, eng):
             t = stage.tile([P, 512, 4], BF16, name="wg", tag="wg", bufs=4, align_bytes=64)
             wg[(i, g, h)] = t
-            src = w_raw[i][:, g, :, 512 * h : 512 * h + 512]
-            evac(
-                eng,
-                t[:].rearrange("p (c i) t -> p c t i", i=4),
-                src.rearrange("p t (c i) -> p c t i", i=4),
-            )
+            regroup(eng, t[:], i, g, 512 * h, 512)
 
-        def quant_w(i, g, h):
+        def RW2(i, g, h, ns):
+            t = stage.tile([P, 512, 4], BF16, name="wg", tag="wg", bufs=4, align_bytes=64)
+            wg[(i, g, h)] = t
+            regroup("V", t[:, 0 : 512 - ns, :], i, g, 512 * h, 512 - ns)
+            regroup("S", t[:, 512 - ns : 512, :], i, g, 512 * h + 512 - ns, ns)
+
+        def QW(i, g, h):
             lo = D * g + 512 * h
             nc.vector.quantize_mx(
                 out=w_cod[i][:, lo : lo + 512].bitcast(FP8X4),
@@ -134,9 +205,9 @@ def tile_graphnet_kernel(tc, X, adj, W_l, W_l1, out):
 
         eg = {}
 
-        def e1_blocks(b, wbs, engs):
+        def E(b, wbs, engs):
             if b not in eg:
-                eg[b] = stage.tile([P, D, 4], BF16, name="eg%d" % b, tag="eg", align_bytes=64)
+                eg[b] = stage.tile([P, D, 4], BF16, name="eg%d" % b, tag="eg", bufs=2, align_bytes=64)
             for c, wb in enumerate(wbs):
                 bank = psum.tile([P, NT, P], F32, name="be", tag="bank")
                 for t in range(NT):
@@ -154,7 +225,7 @@ def tile_graphnet_kernel(tc, X, adj, W_l, W_l1, out):
                         )
                 evac(engs[c], eg[b][:, P * wb : P * wb + P, :], bank[:].rearrange("p t w -> p w t"))
 
-        def quant_e(b, h):
+        def QE(b, h):
             nc.vector.quantize_mx(
                 out=e_cod[b][:, 512 * h : 512 * h + 512].bitcast(FP8X4),
                 scales=e_scl[b][:, 512 * h : 512 * h + 512],
@@ -162,27 +233,56 @@ def tile_graphnet_kernel(tc, X, adj, W_l, W_l1, out):
             )
 
         an = {}
+        rr = {}
 
-        def adj_prep(b):
+        def RS(b):
             rs = stage.tile([P, NT], F32, name="rs", tag="rs")
-            nc.vector.tensor_reduce(out=rs[:], in_=a_raw[b][:], axis=AX.X, op=ALU.add)
+            if RS_ACC:
+                for t in range(NT):
+                    junk = stage.tile([P, N], BF16, name="junk", tag="junk")
+                    nc.vector.tensor_scalar(
+                        out=junk[:], in0=a_raw[b][:, t, :], scalar1=1.0, scalar2=None,
+                        op0=ALU.mult, op1=ALU.add, accum_out=rs[:, t : t + 1],
+                    )
+            else:
+                nc.vector.tensor_reduce(out=rs[:], in_=a_raw[b][:], axis=AX.X, op=ALU.add)
             zm = stage.tile([P, NT], F32, name="zm", tag="zm")
             nc.vector.tensor_scalar(out=zm[:], in0=rs[:], scalar1=0.0, scalar2=None, op0=ALU.is_equal)
             sf = stage.tile([P, NT], F32, name="sf", tag="sf")
             nc.vector.tensor_tensor(out=sf[:], in0=rs[:], in1=zm[:], op=ALU.add)
             rc = stage.tile([P, NT], F32, name="rc", tag="rc")
             nc.vector.reciprocal(out=rc[:], in_=sf[:])
-            rr = stage.tile([P, NT], F32, name="rr", tag="rr")
-            nc.vector.tensor_tensor(out=rr[:], in0=rc[:], in1=zm[:], op=ALU.subtract)
+            rr[b] = stage.tile([P, NT], F32, name="rr%d" % b, tag="rr")
+            nc.vector.tensor_tensor(out=rr[b][:], in0=rc[:], in1=zm[:], op=ALU.subtract)
+
+        def SC(b):
             an[b] = stage.tile([P, NT, N], BF16, name="an%d" % b, tag="an")
             for t in range(NT):
                 nc.vector.tensor_scalar(
-                    out=an[b][:, t, :], in0=a_raw[b][:, t, :], scalar1=rr[:, t : t + 1], scalar2=None, op0=ALU.mult
+                    out=an[b][:, t, :], in0=a_raw[b][:, t, :], scalar1=rr[b][:, t : t + 1], scalar2=None, op0=ALU.mult
+                )
+
+        def SCG(b):
+            an[b] = stage.tile([P, NT, N], BF16, name="an%d" % b, tag="an")
+            for t in range(NT):
+                nc.gpsimd.tensor_scalar(
+                    out=an[b][:, t, :], in0=a_raw[b][:, t, :], scalar1=rr[b][:, t : t + 1], scalar2=0.0,
+                    op0=ALU.mult, op1=ALU.add,
+                )
+
+        def RWG(i, g, h):
+            t = stage.tile([P, 512, 4], BF16, name="wg", tag="wg", bufs=4, align_bytes=64)
+            wg[(i, g, h)] = t
+            for k in range(4):
+                src = w_raw[i][:, g, :, 512 * h + 128 * k : 512 * h + 128 * k + 128]
+                nc.gpsimd.tensor_scalar(
+                    out=t[:, 128 * k : 128 * k + 128, :], in0=src.rearrange("p t c -> p c t"), scalar1=1.0, scalar2=0.0,
+                    op0=ALU.mult, op1=ALU.add,
                 )
 
         ag = {}
 
-        def transpose_a(b, engs):
+        def TA(b, engs):
             ag[b] = stage.tile([P, N, 4], BF16, name="ag%d" % b, tag="ag", align_bytes=64)
             for hi in range(2):
                 bank = psum.tile([P, NT, 256], BF16, name="ba", tag="bank")
@@ -195,95 +295,56 @@ def tile_graphnet_kernel(tc, X, adj, W_l, W_l1, out):
                         )
                 evac(engs[hi], ag[b][:, 256 * hi : 256 * hi + 256, :], bank[:].rearrange("p t i -> p i t"))
 
-        def quant_a(b):
+        def QA(b):
             nc.vector.quantize_mx(
                 out=a_cod[b][:].bitcast(FP8X4), scales=a_scl[b][:], in_=ag[b][:].rearrange("p c t -> p (c t)")
             )
 
-        def out_tiles(b, tis):
-            for ti in tis:
-                res = stage.tile([P, D], F32, name="res", tag="res", bufs=6)
-                for h in range(2):
-                    bank = psum.tile([P, 512], F32, name="bo", tag="bank")
-                    for g in range(G):
-                        xl = N * g + P * ti
-                        wl = D * g + 512 * h
-                        nc.tensor.matmul_mx(
-                            out=bank[:],
-                            lhsT=x_cod[b][:, xl : xl + P].bitcast(FP8X4),
-                            lhsT_scale=x_scl[b][:, xl : xl + P],
-                            rhs=w_cod[0][:, wl : wl + 512].bitcast(FP8X4),
-                            rhs_scale=w_scl[0][:, wl : wl + 512],
-                            start=(g == 0),
-                            stop=False,
-                        )
+        res = {}
+
+        def OP(b, ti, engs="SS"):
+            res[(b, ti)] = stage.tile([P, D], F32, name="res", tag="res", bufs=RES_BUFS)
+            for h in range(2):
+                bank = psum.tile([P, 512], F32, name="bo", tag="bank")
+                for g in range(G):
+                    xl = N * g + P * ti
+                    wl = D * g + 512 * h
                     nc.tensor.matmul_mx(
                         out=bank[:],
-                        lhsT=a_cod[b][:, P * ti : P * ti + P].bitcast(FP8X4),
-                        lhsT_scale=a_scl[b][:, P * ti : P * ti + P],
-                        rhs=e_cod[b][:, 512 * h : 512 * h + 512].bitcast(FP8X4),
-                        rhs_scale=e_scl[b][:, 512 * h : 512 * h + 512],
-                        start=False,
-                        stop=True,
+                        lhsT=x_cod[b][:, xl : xl + P].bitcast(FP8X4),
+                        lhsT_scale=x_scl[b][:, xl : xl + P],
+                        rhs=w_cod[0][:, wl : wl + 512].bitcast(FP8X4),
+                        rhs_scale=w_scl[0][:, wl : wl + 512],
+                        start=(g == 0),
+                        stop=False,
                     )
-                    nc.scalar.copy(out=res[:, 512 * h : 512 * h + 512], in_=bank[:])
-                nc.vector.scalar_tensor_tensor(
-                    out=res[:], in0=res[:], scalar=0.01, in1=res[:], op0=ALU.mult, op1=ALU.max
+                nc.tensor.matmul_mx(
+                    out=bank[:],
+                    lhsT=a_cod[b][:, P * ti : P * ti + P].bitcast(FP8X4),
+                    lhsT_scale=a_scl[b][:, P * ti : P * ti + P],
+                    rhs=e_cod[b][:, 512 * h : 512 * h + 512].bitcast(FP8X4),
+                    rhs_scale=e_scl[b][:, 512 * h : 512 * h + 512],
+                    start=False,
+                    stop=True,
                 )
-                nc.sync.dma_start(out=out[b, P * ti : P * ti + P, :], in_=res[:])
+                evac(engs[h], res[(b, ti)][:, 512 * h : 512 * h + 512], bank[:])
 
-        transpose_x(0, "SSSS")
-        regroup_w(1, 0, 0, "V")
-        regroup_w(1, 1, 0, "S")
-        quant_x(0)
-        quant_w(1, 0, 0)
-        quant_w(1, 1, 0)
-        regroup_w(1, 0, 1, "V")
-        regroup_w(1, 1, 1, "S")
-        e1_blocks(0, [0, 1, 2, 3], "SSSS")
-        quant_w(1, 0, 1)
-        quant_w(1, 1, 1)
-        transpose_x(1, "SSSS")
-        adj_prep(0)
-        e1_blocks(0, [4, 5, 6, 7], "SSSS")
-        quant_x(1)
-        quant_e(0, 0)
-        regroup_w(0, 0, 0, "V")
-        regroup_w(0, 1, 0, "V")
-        quant_e(0, 1)
-        quant_w(0, 0, 0)
-        quant_w(0, 1, 0)
-        e1_blocks(1, [0, 1, 2, 3, 4, 5, 6, 7], "SSSSSSSS")
-        regroup_w(0, 0, 1, "V")
-        regroup_w(0, 1, 1, "V")
-        quant_w(0, 0, 1)
-        quant_w(0, 1, 1)
-        transpose_a(0, "SS")
-        transpose_x(2, "SSSS")
-        quant_e(1, 0)
-        quant_a(0)
-        quant_e(1, 1)
-        quant_x(2)
-        out_tiles(0, [0, 1])
-        adj_prep(1)
-        out_tiles(0, [2, 3])
-        e1_blocks(2, [0, 1, 2, 3, 4, 5, 6, 7], "SSSSSSSS")
-        transpose_a(1, "SS")
-        transpose_x(3, "SSSS")
-        quant_e(2, 0)
-        quant_a(1)
-        quant_e(2, 1)
-        quant_x(3)
-        out_tiles(1, [0, 1])
-        adj_prep(2)
-        out_tiles(1, [2, 3])
-        e1_blocks(3, [0, 1, 2, 3, 4, 5, 6, 7], "SSSSSSSS")
-        adj_prep(3)
-        transpose_a(2, "SS")
-        transpose_a(3, "SS")
-        quant_e(3, 0)
-        quant_a(2)
-        quant_e(3, 1)
-        quant_a(3)
-        out_tiles(2, [0, 1, 2, 3])
-        out_tiles(3, [0, 1, 2, 3])
+        def BS(b, ti, parts=1):
+            r = res[(b, ti)]
+            n = D // parts
+            for k in range(parts):
+                s = r[:, n * k : n * k + n]
+                nc.vector.scalar_tensor_tensor(out=s, in0=s, scalar=0.01, in1=s, op0=ALU.mult, op1=ALU.max)
+                nc.sync.dma_start(out=out[b, P * ti : P * ti + P, n * k : n * k + n], in_=s)
+
+        def O(b, tis):
+            for ti in tis:
+                OP(b, ti)
+                BS(b, ti)
+
+        jobs = {
+            "LX": LX, "LA": LA, "LWC": LWC, "LWP": LWP, "TX": TX, "QX": QX, "RW": RW, "RW2": RW2, "QW": QW,
+            "E": E, "QE": QE, "RS": RS, "SC": SC, "TA": TA, "QA": QA, "O": O, "OP": OP, "BS": BS, "SCG": SCG, "RWG": RWG,
+        }
+        for step in PLAN:
+            jobs[step[0]](*step[1:])

@@ -25,79 +25,286 @@ RES_BUFS = 6
 RS_ACC = True
 
 PLAN = [
-    ("LX",0),
+    ("LX",0,2),
     ("LWC",1,0,0),
     ("LWC",1,0,1),
     ("LWC",1,1,0),
     ("LWC",1,1,1),
     ("LX",1),
+    ("LX",2),
     ("LA",0),
+    ("LX",3),
+    ("LA",1),
     ("LWP",0,0),
     ("LWP",0,1),
-    ("LX",2),
-    ("LA",1),
-    ("LX",3),
     ("LA",2),
     ("LA",3),
-    ("TX",0,"SSSS"),
-    ("RW",1,0,0,"V"),
-    ("RW",1,1,0,"S"),
+    ("TXP",0,0),
+    ("TXP",0,1),
+    ("TXP",0,2),
+    ("TXP",0,3),
+    ("EV","X",0,0,"S"),
+    ("EV","X",0,1,"V"),
+    ("EV","X",0,2,"S"),
+    ("EV","X",0,3,"V"),
     ("QX",0),
+    ("RWp",1,0,0,"V",0,344),
+    ("RWp",1,0,0,"S",344,168),
+    ("RWp",1,1,0,"V",0,344),
+    ("RWp",1,1,0,"S",344,168),
     ("QW",1,0,0),
     ("QW",1,1,0),
-    ("RW",1,0,1,"V"),
-    ("RW",1,1,1,"S"),
-    ("E",0,[0,1,2,3],"SSSS"),
+    ("EP",0,0),
+    ("EV","E",0,0,"S"),
+    ("EP",0,1),
+    ("EV","E",0,1,"S"),
+    ("EP",0,2),
+    ("EV","E",0,2,"S"),
+    ("EP",0,3),
+    ("EV","E",0,3,"S"),
+    ("RWp",1,0,1,"V",0,512),
+    ("RWp",1,1,1,"V",0,512),
     ("QW",1,0,1),
     ("QW",1,1,1),
-    ("TX",1,"SSSS"),
-    ("RS",0),
-    ("SCG",0),
-    ("E",0,[4,5,6,7],"SSSS"),
-    ("QX",1),
+    ("TXP",1,0),
+    ("TXP",1,1),
+    ("TXP",1,2),
+    ("TXP",1,3),
+    ("EV","X",1,0,"S"),
+    ("EV","X",1,1,"V"),
+    ("EV","X",1,2,"S"),
+    ("EV","X",1,3,"V"),
     ("QE",0,0),
-    ("RW",0,0,0,"V"),
-    ("RW",0,1,0,"V"),
+    ("QX",1),
+    ("EP",0,4),
+    ("EV","E",0,4,"S"),
+    ("EP",0,5),
+    ("EV","E",0,5,"S"),
+    ("EP",0,6),
+    ("EV","E",0,6,"S"),
+    ("EP",0,7),
+    ("EV","E",0,7,"S"),
+    ("TXP",2,0),
+    ("TXP",2,1),
+    ("TXP",2,2),
+    ("TXP",2,3),
+    ("EV","X",2,0,"S"),
+    ("EV","X",2,1,"S"),
+    ("EV","X",2,2,"S"),
+    ("EV","X",2,3,"S"),
+    ("RS",0),
+    ("SC",0),
     ("QE",0,1),
-    ("QW",0,0,0),
-    ("QW",0,1,0),
-    ("E",1,[0,1,2,3,4,5,6,7],"SSSSSSSS"),
-    ("RWG",0,0,1),
-    ("RWG",0,1,1),
-    ("QW",0,0,1),
-    ("QW",0,1,1),
-    ("TA",0,"SS"),
-    ("TX",2,"SSSS"),
-    ("QE",1,0),
-    ("QA",0),
-    ("QE",1,1),
+    ("EP",1,0),
+    ("EV","E",1,0,"S"),
+    ("EP",1,1),
+    ("EV","E",1,1,"S"),
+    ("EP",1,2),
+    ("EV","E",1,2,"S"),
+    ("EP",1,3),
+    ("EV","E",1,3,"S"),
     ("QX",2),
-    ("O",0,[0,1]),
+    ("EP",1,4),
+    ("EV","E",1,4,"S"),
+    ("EP",1,5),
+    ("EV","E",1,5,"S"),
+    ("EP",1,6),
+    ("EV","E",1,6,"S"),
+    ("EP",1,7),
+    ("EV","E",1,7,"S"),
+    ("TXP",3,0),
+    ("TXP",3,1),
+    ("TXP",3,2),
+    ("TXP",3,3),
+    ("EV","X",3,0,"S"),
+    ("EV","X",3,1,"S"),
+    ("EV","X",3,2,"S"),
+    ("EV","X",3,3,"S"),
     ("RS",1),
-    ("SCG",1),
-    ("O",0,[2,3]),
-    ("E",2,[0,1,2,3,4,5,6,7],"SSSSSSSS"),
-    ("TA",1,"SS"),
-    ("TX",3,"SSSS"),
-    ("QE",2,0),
-    ("QA",1),
-    ("QE",2,1),
+    ("SC",1),
     ("QX",3),
-    ("O",1,[0,1]),
+    ("EP",2,0),
+    ("EV","E",2,0,"S"),
+    ("EP",2,1),
+    ("EV","E",2,1,"S"),
+    ("EP",2,2),
+    ("EV","E",2,2,"S"),
+    ("EP",2,3),
+    ("EV","E",2,3,"S"),
+    ("TAP",0,0),
+    ("TAP",0,1),
+    ("EV","A",0,0,"S"),
+    ("EV","A",0,1,"S"),
+    ("RWp",0,0,0,"V",0,512),
+    ("RWp",0,0,1,"V",0,512),
+    ("QW",0,0,0),
+    ("QW",0,0,1),
+    ("QA",0),
+    ("EP",2,4),
+    ("EV","E",2,4,"S"),
+    ("EP",2,5),
+    ("EV","E",2,5,"S"),
+    ("EP",2,6),
+    ("EV","E",2,6,"S"),
+    ("EP",2,7),
+    ("EV","E",2,7,"S"),
+    ("RWp",0,1,0,"V",0,512),
+    ("RWp",0,1,1,"V",0,512),
+    ("QW",0,1,0),
+    ("QW",0,1,1),
+    ("EP",3,0),
+    ("EV","E",3,0,"S"),
+    ("EP",3,1),
+    ("EV","E",3,1,"S"),
+    ("EP",3,2),
+    ("EV","E",3,2,"S"),
+    ("EP",3,3),
+    ("EV","E",3,3,"S"),
+    ("TAP",1,0),
+    ("TAP",1,1),
+    ("EV","A",1,0,"S"),
+    ("EV","A",1,1,"S"),
+    ("EP",3,4),
+    ("EV","E",3,4,"S"),
+    ("EP",3,5),
+    ("EV","E",3,5,"S"),
+    ("EP",3,6),
+    ("EV","E",3,6,"S"),
+    ("EP",3,7),
+    ("EV","E",3,7,"S"),
+    ("QE",1,0),
+    ("QE",1,1),
+    ("QA",1),
     ("RS",2),
-    ("SCG",2),
-    ("O",1,[2,3]),
-    ("E",3,[0,1,2,3,4,5,6,7],"SSSSSSSS"),
+    ("SC",2),
+    ("OPX",0,0,0),
+    ("OPE",0,0,0),
+    ("EV","O",0,0,"S"),
+    ("OPX",0,0,1),
+    ("OPE",0,0,1),
+    ("EV","O",0,1,"S"),
+    ("BS",0,0,1),
+    ("OPX",0,1,0),
+    ("OPE",0,1,0),
+    ("EV","O",0,2,"S"),
+    ("OPX",0,1,1),
+    ("OPE",0,1,1),
+    ("EV","O",0,3,"S"),
+    ("BS",0,1,1),
+    ("QE",2,0),
+    ("QE",2,1),
+    ("OPX",0,2,0),
+    ("OPE",0,2,0),
+    ("EV","O",0,4,"S"),
+    ("OPX",0,2,1),
+    ("OPE",0,2,1),
+    ("EV","O",0,5,"S"),
+    ("BS",0,2,1),
+    ("OPX",0,3,0),
+    ("OPE",0,3,0),
+    ("EV","O",0,6,"S"),
+    ("OPX",0,3,1),
+    ("OPE",0,3,1),
+    ("EV","O",0,7,"S"),
+    ("BS",0,3,1),
     ("RS",3),
-    ("SCG",3),
-    ("TA",2,"SS"),
-    ("TA",3,"SS"),
-    ("QE",3,0),
+    ("SC",3),
+    ("TAP",2,0),
+    ("TAP",2,1),
+    ("EV","A",2,0,"S"),
+    ("EV","A",2,1,"S"),
+    ("OPX",1,0,0),
+    ("OPE",1,0,0),
+    ("EV","O",1,0,"S"),
+    ("OPX",1,0,1),
+    ("OPE",1,0,1),
+    ("EV","O",1,1,"S"),
+    ("BS",1,0,1),
+    ("OPX",1,1,0),
+    ("OPE",1,1,0),
+    ("EV","O",1,2,"S"),
+    ("OPX",1,1,1),
+    ("OPE",1,1,1),
+    ("EV","O",1,3,"S"),
+    ("BS",1,1,1),
     ("QA",2),
+    ("QE",3,0),
+    ("OPX",1,2,0),
+    ("OPE",1,2,0),
+    ("EV","O",1,4,"S"),
+    ("OPX",1,2,1),
+    ("OPE",1,2,1),
+    ("EV","O",1,5,"S"),
+    ("BS",1,2,1),
+    ("OPX",1,3,0),
+    ("OPE",1,3,0),
+    ("EV","O",1,6,"S"),
+    ("OPX",1,3,1),
+    ("OPE",1,3,1),
+    ("EV","O",1,7,"S"),
+    ("BS",1,3,1),
     ("QE",3,1),
+    ("TAP",3,0),
+    ("TAP",3,1),
+    ("EV","A",3,0,"S"),
+    ("EV","A",3,1,"S"),
+    ("OPX",2,0,0),
+    ("OPE",2,0,0),
+    ("EV","O",2,0,"S"),
+    ("OPX",2,0,1),
+    ("OPE",2,0,1),
+    ("EV","O",2,1,"S"),
+    ("BS",2,0,1),
+    ("OPX",2,1,0),
+    ("OPE",2,1,0),
+    ("EV","O",2,2,"S"),
+    ("OPX",2,1,1),
+    ("OPE",2,1,1),
+    ("EV","O",2,3,"S"),
+    ("BS",2,1,1),
     ("QA",3),
-    ("O",2,[0,1,2,3]),
-    ("O",3,[0,1,2,3]),
+    ("OPX",2,2,0),
+    ("OPE",2,2,0),
+    ("EV","O",2,4,"S"),
+    ("OPX",2,2,1),
+    ("OPE",2,2,1),
+    ("EV","O",2,5,"S"),
+    ("BS",2,2,1),
+    ("OPX",2,3,0),
+    ("OPE",2,3,0),
+    ("EV","O",2,6,"S"),
+    ("OPX",2,3,1),
+    ("OPE",2,3,1),
+    ("EV","O",2,7,"S"),
+    ("BS",2,3,1),
+    ("OPX",3,0,0),
+    ("OPE",3,0,0),
+    ("EV","O",3,0,"S"),
+    ("OPX",3,0,1),
+    ("OPE",3,0,1),
+    ("EV","O",3,1,"S"),
+    ("BS",3,0,1),
+    ("OPX",3,1,0),
+    ("OPE",3,1,0),
+    ("EV","O",3,2,"S"),
+    ("OPX",3,1,1),
+    ("OPE",3,1,1),
+    ("EV","O",3,3,"S"),
+    ("BS",3,1,1),
+    ("OPX",3,2,0),
+    ("OPE",3,2,0),
+    ("EV","O",3,4,"S"),
+    ("OPX",3,2,1),
+    ("OPE",3,2,1),
+    ("EV","O",3,5,"S"),
+    ("BS",3,2,1),
+    ("OPX",3,3,0),
+    ("OPE",3,3,0),
+    ("EV","O",3,6,"S"),
+    ("OPX",3,3,1),
+    ("OPE",3,3,1),
+    ("EV","O",3,7,"S"),
+    ("BS",3,3,2),
 ]
 
 
@@ -117,15 +324,15 @@ def tile_graphnet_kernel(tc, X, adj, W_l, W_l1, out):
 
         x_raw = [keep.tile([P, NT * D], BF16, name="x_raw%d" % b, tag="x_raw", bufs=3) for b in range(B)]
         a_raw = [keep.tile([P, NT, N], BF16, name="a_raw%d" % b) for b in range(B)]
-        w_raw = [keep.tile([P, G, 4, D], BF16, name="w_raw%d" % i) for i in range(2)]
+        w_raw = {}
         x_cod = [keep.tile([P, G * N], U32, name="x_cod%d" % b, align_bytes=64) for b in range(B)]
         x_scl = [keep.tile([P, G * N], U8, name="x_scl%d" % b, align_bytes=64) for b in range(B)]
         w_cod = [keep.tile([P, G * D], U32, name="w_cod%d" % i, align_bytes=64) for i in range(2)]
         w_scl = [keep.tile([P, G * D], U8, name="w_scl%d" % i, align_bytes=64) for i in range(2)]
         a_cod = [keep.tile([P, N], U32, name="a_cod%d" % b, align_bytes=64) for b in range(B)]
         a_scl = [keep.tile([P, N], U8, name="a_scl%d" % b, align_bytes=64) for b in range(B)]
-        e_cod = [keep.tile([P, D], U32, name="e_cod%d" % b, tag="e_cod", bufs=3, align_bytes=64) for b in range(B)]
-        e_scl = [keep.tile([P, D], U8, name="e_scl%d" % b, tag="e_scl", bufs=3, align_bytes=64) for b in range(B)]
+        e_cod = [keep.tile([P, D], U32, name="e_cod%d" % b, tag="e_cod", bufs=4, align_bytes=64) for b in range(B)]
+        e_scl = [keep.tile([P, D], U8, name="e_scl%d" % b, tag="e_scl", bufs=4, align_bytes=64) for b in range(B)]
         W = [W_l, W_l1]
 
         def LX(b, parts=1):
@@ -138,15 +345,20 @@ def tile_graphnet_kernel(tc, X, adj, W_l, W_l1, out):
         def LA(b):
             nc.sync.dma_start(out=a_raw[b][:], in_=adj[b].rearrange("(t p) j -> p t j", p=P))
 
+        def raw_w(i):
+            if i not in w_raw:
+                w_raw[i] = keep.tile([P, G, 4, D], BF16, name="w_raw%d" % i, tag="w_raw", bufs=1)
+            return w_raw[i]
+
         def LWC(i, h, e):
-            dst = w_raw[i][:].rearrange("p g (u e) n -> p (g u) e n", e=2)
+            dst = raw_w(i)[:].rearrange("p g (u e) n -> p (g u) e n", e=2)
             src = W[i].rearrange("(q p e) n -> p q e n", q=4, p=P, e=2)
             nc.sync.dma_start(
                 out=dst[:, :, e, 512 * h : 512 * h + 512], in_=src[:, :, e, 512 * h : 512 * h + 512]
             )
 
         def LWP(i, g):
-            dst = w_raw[i][:, g].rearrange("p (u e) n -> p u e n", e=2)
+            dst = raw_w(i)[:, g].rearrange("p (u e) n -> p u e n", e=2)
             src = W[i][512 * g : 512 * g + 512, :].rearrange("(u p e) n -> p u e n", u=2, p=P, e=2)
             nc.sync.dma_start(out=dst, in_=src)
 
@@ -207,7 +419,7 @@ def tile_graphnet_kernel(tc, X, adj, W_l, W_l1, out):
 
         def E(b, wbs, engs):
             if b not in eg:
-                eg[b] = stage.tile([P, D, 4], BF16, name="eg%d" % b, tag="eg", bufs=2, align_bytes=64)
+                eg[b] = stage.tile([P, D, 4], BF16, name="eg%d" % b, tag="eg", bufs=3, align_bytes=64)
             for c, wb in enumerate(wbs):
                 bank = psum.tile([P, NT, P], F32, name="be", tag="bank")
                 for t in range(NT):
@@ -342,7 +554,104 @@ def tile_graphnet_kernel(tc, X, adj, W_l, W_l1, out):
                 OP(b, ti)
                 BS(b, ti)
 
+        banks = {}
+
+        def TXP(b, c):
+            if c == 0:
+                xg[b] = stage.tile([P, G * N * 4], BF16, name="xg%d" % b, tag="xg", align_bytes=64)
+            hn = c // 2
+            g = c % 2
+            xw = x_raw[b][:].bitcast(F32)
+            bank = psum.tile([P, 2, 256], F32, name="bx", tag="bank")
+            banks[("X", b, c)] = bank
+            for u in range(2):
+                for tt in range(2):
+                    col = 512 * (2 * hn + tt) + 256 * g + 128 * u
+                    nc.tensor.transpose(bank[:, u, 128 * tt : 128 * tt + 128], xw[:, col : col + 128], ident_f[:])
+
+        def EP(b, wb):
+            if b not in eg:
+                eg[b] = stage.tile([P, D, 4], BF16, name="eg%d" % b, tag="eg", bufs=3, align_bytes=64)
+            bank = psum.tile([P, NT, P], F32, name="be", tag="bank")
+            banks[("E", b, wb)] = bank
+            for t in range(NT):
+                for g in range(G):
+                    xl = N * g + P * t
+                    wl = D * g + P * wb
+                    nc.tensor.matmul_mx(
+                        out=bank[:, t, :],
+                        lhsT=x_cod[b][:, xl : xl + P].bitcast(FP8X4),
+                        lhsT_scale=x_scl[b][:, xl : xl + P],
+                        rhs=w_cod[1][:, wl : wl + P].bitcast(FP8X4),
+                        rhs_scale=w_scl[1][:, wl : wl + P],
+                        start=(g == 0),
+                        stop=(g == G - 1),
+                    )
+
+        def TAP(b, hi):
+            if hi == 0:
+                ag[b] = stage.tile([P, N, 4], BF16, name="ag%d" % b, tag="ag", align_bytes=64)
+            bank = psum.tile([P, NT, 256], BF16, name="ba", tag="bank")
+            banks[("A", b, hi)] = bank
+            for tj in range(NT):
+                for ii in range(2):
+                    nc.tensor.transpose(
+                        bank[:, tj, 128 * ii : 128 * ii + 128],
+                        an[b][:, 2 * hi + ii, 128 * tj : 128 * tj + 128],
+                        ident_b[:],
+                    )
+
+        def OPX(b, ti, h):
+            if h == 0:
+                res[(b, ti)] = stage.tile([P, D], F32, name="res", tag="res", bufs=RES_BUFS)
+            bank = psum.tile([P, 512], F32, name="bo", tag="bank")
+            banks[("O", b, 2 * ti + h)] = bank
+            for g in range(G):
+                xl = N * g + P * ti
+                wl = D * g + 512 * h
+                nc.tensor.matmul_mx(
+                    out=bank[:],
+                    lhsT=x_cod[b][:, xl : xl + P].bitcast(FP8X4),
+                    lhsT_scale=x_scl[b][:, xl : xl + P],
+                    rhs=w_cod[0][:, wl : wl + 512].bitcast(FP8X4),
+                    rhs_scale=w_scl[0][:, wl : wl + 512],
+                    start=(g == 0),
+                    stop=False,
+                )
+
+        def OPE(b, ti, h):
+            bank = banks[("O", b, 2 * ti + h)]
+            nc.tensor.matmul_mx(
+                out=bank[:],
+                lhsT=a_cod[b][:, P * ti : P * ti + P].bitcast(FP8X4),
+                lhsT_scale=a_scl[b][:, P * ti : P * ti + P],
+                rhs=e_cod[b][:, 512 * h : 512 * h + 512].bitcast(FP8X4),
+                rhs_scale=e_scl[b][:, 512 * h : 512 * h + 512],
+                start=False,
+                stop=True,
+            )
+
+        def EV(kind, b, c, eng):
+            bank = banks[(kind, b, c)]
+            if kind == "X":
+                dst = xg[b][:].bitcast(F32).rearrange("p (g n u) -> p g n u", g=G, u=2)
+                hn = c // 2
+                evac(eng, dst[:, c % 2, 256 * hn : 256 * hn + 256, :], bank[:].rearrange("p u n -> p n u"))
+            elif kind == "E":
+                evac(eng, eg[b][:, P * c : P * c + P, :], bank[:].rearrange("p t w -> p w t"))
+            elif kind == "A":
+                evac(eng, ag[b][:, 256 * c : 256 * c + 256, :], bank[:].rearrange("p t i -> p i t"))
+            else:
+                h = c % 2
+                evac(eng, res[(b, c // 2)][:, 512 * h : 512 * h + 512], bank[:])
+
+        def RWp(i, g, h, eng, lo, n):
+            if (i, g, h) not in wg:
+                wg[(i, g, h)] = stage.tile([P, 512, 4], BF16, name="wg", tag="wg", bufs=4, align_bytes=64)
+            regroup(eng, wg[(i, g, h)][:, lo : lo + n, :], i, g, 512 * h + lo, n)
+
         jobs = {
+            "TXP": TXP, "EP": EP, "TAP": TAP, "OPX": OPX, "OPE": OPE, "EV": EV, "RWp": RWp,
             "LX": LX, "LA": LA, "LWC": LWC, "LWP": LWP, "TX": TX, "QX": QX, "RW": RW, "RW2": RW2, "QW": QW,
             "E": E, "QE": QE, "RS": RS, "SC": SC, "TA": TA, "QA": QA, "O": O, "OP": OP, "BS": BS, "SCG": SCG, "RWG": RWG,
         }

@@ -9,651 +9,297 @@ U32 = mybir.dt.uint32
 U8 = mybir.dt.uint8
 FP8X4 = mybir.dt.float8_e4m3fn_x4
 ALU = mybir.AluOpType
-AX = mybir.AxisListType
 
 P = 128
-B = 4
-N = 512
-D = 1024
-NT = N // P
-G = D // 512
+PACK = 4
+GRAPHS = 4
+NODES = 512
+FEATS = 1024
+NODE_TILES = NODES // P
+PASSES = FEATS // (P * PACK)
+BANK = 512
+SLOPE = 0.01
 
-FLOPS = 2 * (B * N) * D * D * 2 + 2 * B * N * N * D
+W_OUT = 0
+W_E1 = 1
 
-MANUAL = True
-RES_BUFS = 6
-RS_ACC = True
+SCALAR_SHARE = 88
 
-PLAN = [
-    ("LX",0,2),
-    ("LWC",1,0,0),
-    ("LWC",1,0,1),
-    ("LWC",1,1,0),
-    ("LWC",1,1,1),
-    ("LX",1),
-    ("LX",2),
-    ("LA",0),
-    ("LX",3),
-    ("LA",1),
-    ("LWP",0,0),
-    ("LWP",0,1),
-    ("LA",2),
-    ("LA",3),
-    ("TXP",0,0),
-    ("TXP",0,1),
-    ("TXP",0,2),
-    ("TXP",0,3),
-    ("EV","X",0,0,"S"),
-    ("EV","X",0,1,"V"),
-    ("EV","X",0,2,"S"),
-    ("EV","X",0,3,"V"),
-    ("QX",0),
-    ("RWp",1,0,0,"V",0,344),
-    ("RWp",1,0,0,"S",344,168),
-    ("RWp",1,1,0,"V",0,344),
-    ("RWp",1,1,0,"S",344,168),
-    ("QW",1,0,0),
-    ("QW",1,1,0),
-    ("EP",0,0),
-    ("EV","E",0,0,"S"),
-    ("EP",0,1),
-    ("EV","E",0,1,"S"),
-    ("EP",0,2),
-    ("EV","E",0,2,"S"),
-    ("EP",0,3),
-    ("EV","E",0,3,"S"),
-    ("RWp",1,0,1,"V",0,512),
-    ("RWp",1,1,1,"V",0,512),
-    ("QW",1,0,1),
-    ("QW",1,1,1),
-    ("TXP",1,0),
-    ("TXP",1,1),
-    ("TXP",1,2),
-    ("TXP",1,3),
-    ("EV","X",1,0,"S"),
-    ("EV","X",1,1,"V"),
-    ("EV","X",1,2,"S"),
-    ("EV","X",1,3,"V"),
-    ("QE",0,0),
-    ("QX",1),
-    ("EP",0,4),
-    ("EV","E",0,4,"S"),
-    ("EP",0,5),
-    ("EV","E",0,5,"S"),
-    ("EP",0,6),
-    ("EV","E",0,6,"S"),
-    ("EP",0,7),
-    ("EV","E",0,7,"S"),
-    ("TXP",2,0),
-    ("TXP",2,1),
-    ("TXP",2,2),
-    ("TXP",2,3),
-    ("EV","X",2,0,"S"),
-    ("EV","X",2,1,"S"),
-    ("EV","X",2,2,"S"),
-    ("EV","X",2,3,"S"),
-    ("RS",0),
-    ("SC",0),
-    ("QE",0,1),
-    ("EP",1,0),
-    ("EV","E",1,0,"S"),
-    ("EP",1,1),
-    ("EV","E",1,1,"S"),
-    ("EP",1,2),
-    ("EV","E",1,2,"S"),
-    ("EP",1,3),
-    ("EV","E",1,3,"S"),
-    ("QX",2),
-    ("EP",1,4),
-    ("EV","E",1,4,"S"),
-    ("EP",1,5),
-    ("EV","E",1,5,"S"),
-    ("EP",1,6),
-    ("EV","E",1,6,"S"),
-    ("EP",1,7),
-    ("EV","E",1,7,"S"),
-    ("TXP",3,0),
-    ("TXP",3,1),
-    ("TXP",3,2),
-    ("TXP",3,3),
-    ("EV","X",3,0,"S"),
-    ("EV","X",3,1,"S"),
-    ("EV","X",3,2,"S"),
-    ("EV","X",3,3,"S"),
-    ("RS",1),
-    ("SC",1),
-    ("QX",3),
-    ("EP",2,0),
-    ("EV","E",2,0,"S"),
-    ("EP",2,1),
-    ("EV","E",2,1,"S"),
-    ("EP",2,2),
-    ("EV","E",2,2,"S"),
-    ("EP",2,3),
-    ("EV","E",2,3,"S"),
-    ("TAP",0,0),
-    ("TAP",0,1),
-    ("EV","A",0,0,"S"),
-    ("EV","A",0,1,"S"),
-    ("RWp",0,0,0,"V",0,512),
-    ("RWp",0,0,1,"V",0,512),
-    ("QW",0,0,0),
-    ("QW",0,0,1),
-    ("QA",0),
-    ("EP",2,4),
-    ("EV","E",2,4,"S"),
-    ("EP",2,5),
-    ("EV","E",2,5,"S"),
-    ("EP",2,6),
-    ("EV","E",2,6,"S"),
-    ("EP",2,7),
-    ("EV","E",2,7,"S"),
-    ("RWp",0,1,0,"V",0,512),
-    ("RWp",0,1,1,"V",0,512),
-    ("QW",0,1,0),
-    ("QW",0,1,1),
-    ("EP",3,0),
-    ("EV","E",3,0,"S"),
-    ("EP",3,1),
-    ("EV","E",3,1,"S"),
-    ("EP",3,2),
-    ("EV","E",3,2,"S"),
-    ("EP",3,3),
-    ("EV","E",3,3,"S"),
-    ("TAP",1,0),
-    ("TAP",1,1),
-    ("EV","A",1,0,"S"),
-    ("EV","A",1,1,"S"),
-    ("EP",3,4),
-    ("EV","E",3,4,"S"),
-    ("EP",3,5),
-    ("EV","E",3,5,"S"),
-    ("EP",3,6),
-    ("EV","E",3,6,"S"),
-    ("EP",3,7),
-    ("EV","E",3,7,"S"),
-    ("QE",1,0),
-    ("QE",1,1),
-    ("QA",1),
-    ("RS",2),
-    ("SC",2),
-    ("OPX",0,0,0),
-    ("OPE",0,0,0),
-    ("EV","O",0,0,"S"),
-    ("OPX",0,0,1),
-    ("OPE",0,0,1),
-    ("EV","O",0,1,"S"),
-    ("BS",0,0,1),
-    ("OPX",0,1,0),
-    ("OPE",0,1,0),
-    ("EV","O",0,2,"S"),
-    ("OPX",0,1,1),
-    ("OPE",0,1,1),
-    ("EV","O",0,3,"S"),
-    ("BS",0,1,1),
-    ("QE",2,0),
-    ("QE",2,1),
-    ("OPX",0,2,0),
-    ("OPE",0,2,0),
-    ("EV","O",0,4,"S"),
-    ("OPX",0,2,1),
-    ("OPE",0,2,1),
-    ("EV","O",0,5,"S"),
-    ("BS",0,2,1),
-    ("OPX",0,3,0),
-    ("OPE",0,3,0),
-    ("EV","O",0,6,"S"),
-    ("OPX",0,3,1),
-    ("OPE",0,3,1),
-    ("EV","O",0,7,"S"),
-    ("BS",0,3,1),
-    ("RS",3),
-    ("SC",3),
-    ("TAP",2,0),
-    ("TAP",2,1),
-    ("EV","A",2,0,"S"),
-    ("EV","A",2,1,"S"),
-    ("OPX",1,0,0),
-    ("OPE",1,0,0),
-    ("EV","O",1,0,"S"),
-    ("OPX",1,0,1),
-    ("OPE",1,0,1),
-    ("EV","O",1,1,"S"),
-    ("BS",1,0,1),
-    ("OPX",1,1,0),
-    ("OPE",1,1,0),
-    ("EV","O",1,2,"S"),
-    ("OPX",1,1,1),
-    ("OPE",1,1,1),
-    ("EV","O",1,3,"S"),
-    ("BS",1,1,1),
-    ("QA",2),
-    ("QE",3,0),
-    ("OPX",1,2,0),
-    ("OPE",1,2,0),
-    ("EV","O",1,4,"S"),
-    ("OPX",1,2,1),
-    ("OPE",1,2,1),
-    ("EV","O",1,5,"S"),
-    ("BS",1,2,1),
-    ("OPX",1,3,0),
-    ("OPE",1,3,0),
-    ("EV","O",1,6,"S"),
-    ("OPX",1,3,1),
-    ("OPE",1,3,1),
-    ("EV","O",1,7,"S"),
-    ("BS",1,3,1),
-    ("QE",3,1),
-    ("TAP",3,0),
-    ("TAP",3,1),
-    ("EV","A",3,0,"S"),
-    ("EV","A",3,1,"S"),
-    ("OPX",2,0,0),
-    ("OPE",2,0,0),
-    ("EV","O",2,0,"S"),
-    ("OPX",2,0,1),
-    ("OPE",2,0,1),
-    ("EV","O",2,1,"S"),
-    ("BS",2,0,1),
-    ("OPX",2,1,0),
-    ("OPE",2,1,0),
-    ("EV","O",2,2,"S"),
-    ("OPX",2,1,1),
-    ("OPE",2,1,1),
-    ("EV","O",2,3,"S"),
-    ("BS",2,1,1),
-    ("QA",3),
-    ("OPX",2,2,0),
-    ("OPE",2,2,0),
-    ("EV","O",2,4,"S"),
-    ("OPX",2,2,1),
-    ("OPE",2,2,1),
-    ("EV","O",2,5,"S"),
-    ("BS",2,2,1),
-    ("OPX",2,3,0),
-    ("OPE",2,3,0),
-    ("EV","O",2,6,"S"),
-    ("OPX",2,3,1),
-    ("OPE",2,3,1),
-    ("EV","O",2,7,"S"),
-    ("BS",2,3,1),
-    ("OPX",3,0,0),
-    ("OPE",3,0,0),
-    ("EV","O",3,0,"S"),
-    ("OPX",3,0,1),
-    ("OPE",3,0,1),
-    ("EV","O",3,1,"S"),
-    ("BS",3,0,1),
-    ("OPX",3,1,0),
-    ("OPE",3,1,0),
-    ("EV","O",3,2,"S"),
-    ("OPX",3,1,1),
-    ("OPE",3,1,1),
-    ("EV","O",3,3,"S"),
-    ("BS",3,1,1),
-    ("OPX",3,2,0),
-    ("OPE",3,2,0),
-    ("EV","O",3,4,"S"),
-    ("OPX",3,2,1),
-    ("OPE",3,2,1),
-    ("EV","O",3,5,"S"),
-    ("BS",3,2,1),
-    ("OPX",3,3,0),
-    ("OPE",3,3,0),
-    ("EV","O",3,6,"S"),
-    ("OPX",3,3,1),
-    ("OPE",3,3,1),
-    ("EV","O",3,7,"S"),
-    ("BS",3,3,2),
-]
+WAITING_COLUMNS = 1024
+
+FLOPS = 2 * (GRAPHS * NODES) * FEATS * FEATS * 2 + 2 * GRAPHS * NODES * NODES * FEATS
 
 
 def tile_graphnet_kernel(tc, X, adj, W_l, W_l1, out):
     nc = tc.nc
+    weights = [W_l, W_l1]
     with ExitStack() as ctx:
-        if MANUAL:
-            ctx.enter_context(tc.manual_schedule())
+        ctx.enter_context(tc.manual_schedule())
         keep = ctx.enter_context(tc.tile_pool(name="keep", bufs=1))
         stage = ctx.enter_context(tc.tile_pool(name="stage", bufs=2))
         psum = ctx.enter_context(tc.psum_pool(name="psum", bufs=8))
 
-        ident_f = keep.tile([P, P], F32, name="ident_f")
-        make_identity(nc, ident_f[:])
-        ident_b = keep.tile([P, P], BF16, name="ident_b")
-        make_identity(nc, ident_b[:])
+        ident_f32 = keep.tile([P, P], F32, name="ident_f32")
+        make_identity(nc, ident_f32[:])
+        ident_bf16 = keep.tile([P, P], BF16, name="ident_bf16")
+        make_identity(nc, ident_bf16[:])
 
-        x_raw = [keep.tile([P, NT * D], BF16, name="x_raw%d" % b, tag="x_raw", bufs=3) for b in range(B)]
-        a_raw = [keep.tile([P, NT, N], BF16, name="a_raw%d" % b) for b in range(B)]
+        x_raw = [keep.tile([P, NODE_TILES * FEATS], BF16, name="x_raw%d" % b, tag="x_raw", bufs=3) for b in range(GRAPHS)]
+        adj_raw = [keep.tile([P, NODE_TILES, NODES], BF16, name="adj_raw%d" % b) for b in range(GRAPHS)]
         w_raw = {}
-        x_cod = [keep.tile([P, G * N], U32, name="x_cod%d" % b, align_bytes=64) for b in range(B)]
-        x_scl = [keep.tile([P, G * N], U8, name="x_scl%d" % b, align_bytes=64) for b in range(B)]
-        w_cod = [keep.tile([P, G * D], U32, name="w_cod%d" % i, align_bytes=64) for i in range(2)]
-        w_scl = [keep.tile([P, G * D], U8, name="w_scl%d" % i, align_bytes=64) for i in range(2)]
-        a_cod = [keep.tile([P, N], U32, name="a_cod%d" % b, align_bytes=64) for b in range(B)]
-        a_scl = [keep.tile([P, N], U8, name="a_scl%d" % b, align_bytes=64) for b in range(B)]
-        e_cod = [keep.tile([P, D], U32, name="e_cod%d" % b, tag="e_cod", bufs=4, align_bytes=64) for b in range(B)]
-        e_scl = [keep.tile([P, D], U8, name="e_scl%d" % b, tag="e_scl", bufs=4, align_bytes=64) for b in range(B)]
-        W = [W_l, W_l1]
 
-        def LX(b, parts=1):
-            dst = x_raw[b][:].rearrange("p (t d) -> p t d", t=NT)
+        def operand(name, columns):
+            words = keep.tile([P, columns], U32, name=name + "_words", align_bytes=64)
+            plane = keep.tile([P, columns], U8, name=name + "_plane", align_bytes=64)
+            return words, plane
+
+        x_q = [operand("x%d" % b, PASSES * NODES) for b in range(GRAPHS)]
+        w_q = [operand("w%d" % i, PASSES * FEATS) for i in range(2)]
+        adj_q = [operand("adj%d" % b, NODES) for b in range(GRAPHS)]
+        e1_q = [operand("e1_%d" % b, FEATS) for b in range(GRAPHS)]
+
+        def quantise(operand_q, lo, n, grouped):
+            words, plane = operand_q
+            nc.vector.quantize_mx(out=words[:, lo : lo + n].bitcast(FP8X4), scales=plane[:, lo : lo + n], in_=grouped)
+
+        def mx_pass(acc, lhs_q, lhs_lo, rhs_q, rhs_lo, n, start, stop):
+            nc.tensor.matmul_mx(
+                out=acc,
+                lhsT=lhs_q[0][:, lhs_lo : lhs_lo + P].bitcast(FP8X4),
+                lhsT_scale=lhs_q[1][:, lhs_lo : lhs_lo + P],
+                rhs=rhs_q[0][:, rhs_lo : rhs_lo + n].bitcast(FP8X4),
+                rhs_scale=rhs_q[1][:, rhs_lo : rhs_lo + n],
+                start=start,
+                stop=stop,
+            )
+
+        def by_scalar(dst, src):
+            nc.scalar.copy(out=dst, in_=src)
+
+        def by_vector(dst, src):
+            nc.vector.tensor_copy(out=dst, in_=src)
+
+        def load_x(b, pieces):
+            dst = x_raw[b][:].rearrange("p (t d) -> p t d", t=NODE_TILES)
             src = X[b].rearrange("(t p) d -> p t d", p=P)
-            n = NT // parts
-            for k in range(parts):
+            n = NODE_TILES // pieces
+            for k in range(pieces):
                 nc.sync.dma_start(out=dst[:, n * k : n * k + n, :], in_=src[:, n * k : n * k + n, :])
 
-        def LA(b):
-            nc.sync.dma_start(out=a_raw[b][:], in_=adj[b].rearrange("(t p) j -> p t j", p=P))
+        def load_adj(b):
+            nc.sync.dma_start(out=adj_raw[b][:], in_=adj[b].rearrange("(t p) j -> p t j", p=P))
 
-        def raw_w(i):
+        def raw_weight(i):
             if i not in w_raw:
-                w_raw[i] = keep.tile([P, G, 4, D], BF16, name="w_raw%d" % i, tag="w_raw", bufs=1)
+                w_raw[i] = keep.tile([P, PASSES, PACK, FEATS], BF16, name="w_raw%d" % i, tag="w_raw")
             return w_raw[i]
 
-        def LWC(i, h, e):
-            dst = raw_w(i)[:].rearrange("p g (u e) n -> p (g u) e n", e=2)
-            src = W[i].rearrange("(q p e) n -> p q e n", q=4, p=P, e=2)
-            nc.sync.dma_start(
-                out=dst[:, :, e, 512 * h : 512 * h + 512], in_=src[:, :, e, 512 * h : 512 * h + 512]
-            )
+        def load_weight_columns(i, lo, n):
+            dst = raw_weight(i)[:].rearrange("p g (u e) c -> p (g u) e c", e=2)
+            src = weights[i].rearrange("(q p e) c -> p q e c", p=P, e=2)
+            for e in range(2):
+                nc.sync.dma_start(out=dst[:, :, e, lo : lo + n], in_=src[:, :, e, lo : lo + n])
 
-        def LWP(i, g):
-            dst = raw_w(i)[:, g].rearrange("p (u e) n -> p u e n", e=2)
-            src = W[i][512 * g : 512 * g + 512, :].rearrange("(u p e) n -> p u e n", u=2, p=P, e=2)
-            nc.sync.dma_start(out=dst, in_=src)
+        def load_weight_pass(i, g):
+            dst = raw_weight(i)[:, g].rearrange("p (u e) c -> p u e c", e=2)
+            rows = weights[i][P * PACK * g : P * PACK * (g + 1), :]
+            nc.sync.dma_start(out=dst, in_=rows.rearrange("(u p e) c -> p u e c", p=P, e=2))
 
-        def evac(eng, dst, src):
-            if eng == "S":
-                nc.scalar.copy(out=dst, in_=src)
-            else:
-                nc.vector.tensor_copy(out=dst, in_=src)
+        x_grouped = {}
 
-        xg = {}
-
-        def TX(b, engs):
-            xg[b] = stage.tile([P, G * N * 4], BF16, name="xg%d" % b, tag="xg", align_bytes=64)
-            xw = x_raw[b][:].bitcast(F32)
-            dst = xg[b][:].bitcast(F32).rearrange("p (g n u) -> p g n u", g=G, u=2)
-            c = 0
-            for hn in range(2):
-                for g in range(G):
-                    bank = psum.tile([P, 2, 256], F32, name="bx", tag="bank")
+        def transpose_x(b, copiers):
+            x_grouped[b] = stage.tile([P, PASSES * NODES * PACK], BF16, name="x_grouped%d" % b, tag="x_grouped", align_bytes=64)
+            words = x_raw[b][:].bitcast(F32)
+            dst = x_grouped[b][:].bitcast(F32).rearrange("p (g n u) -> p g n u", g=PASSES, u=2)
+            filled = []
+            for half in range(2):
+                for g in range(PASSES):
+                    bank = psum.tile([P, 2, 2 * P], F32, name="x_bank", tag="bank")
                     for u in range(2):
-                        for tt in range(2):
-                            col = 512 * (2 * hn + tt) + 256 * g + 128 * u
-                            nc.tensor.transpose(
-                                bank[:, u, 128 * tt : 128 * tt + 128], xw[:, col : col + 128], ident_f[:]
-                            )
-                    evac(engs[c], dst[:, g, 256 * hn : 256 * hn + 256, :], bank[:].rearrange("p u n -> p n u"))
-                    c += 1
+                        for t in range(2):
+                            lo = (FEATS // 2) * (2 * half + t) + 2 * P * g + P * u
+                            nc.tensor.transpose(bank[:, u, P * t : P * t + P], words[:, lo : lo + P], ident_f32[:])
+                    filled.append((bank, dst[:, g, 2 * P * half : 2 * P * (half + 1), :]))
+            for copier, (bank, where) in zip(copiers, filled):
+                copier(where, bank[:].rearrange("p u n -> p n u"))
 
-        def QX(b):
-            nc.vector.quantize_mx(out=x_cod[b][:].bitcast(FP8X4), scales=x_scl[b][:], in_=xg[b][:])
+        def quantise_x(b):
+            quantise(x_q[b], 0, PASSES * NODES, x_grouped[b][:])
 
-        wg = {}
+        w_grouped = {}
 
-        def regroup(eng, t, i, g, lo, n):
-            src = w_raw[i][:, g, :, lo : lo + n]
-            evac(eng, t.rearrange("p (c i) t -> p c t i", i=4), src.rearrange("p t (c i) -> p c t i", i=4))
-
-        def RW(i, g, h, eng):
-            t = stage.tile([P, 512, 4], BF16, name="wg", tag="wg", bufs=4, align_bytes=64)
-            wg[(i, g, h)] = t
-            regroup(eng, t[:], i, g, 512 * h, 512)
-
-        def RW2(i, g, h, ns):
-            t = stage.tile([P, 512, 4], BF16, name="wg", tag="wg", bufs=4, align_bytes=64)
-            wg[(i, g, h)] = t
-            regroup("V", t[:, 0 : 512 - ns, :], i, g, 512 * h, 512 - ns)
-            regroup("S", t[:, 512 - ns : 512, :], i, g, 512 * h + 512 - ns, ns)
-
-        def QW(i, g, h):
-            lo = D * g + 512 * h
-            nc.vector.quantize_mx(
-                out=w_cod[i][:, lo : lo + 512].bitcast(FP8X4),
-                scales=w_scl[i][:, lo : lo + 512],
-                in_=wg[(i, g, h)][:].rearrange("p c t -> p (c t)"),
-            )
-
-        eg = {}
-
-        def E(b, wbs, engs):
-            if b not in eg:
-                eg[b] = stage.tile([P, D, 4], BF16, name="eg%d" % b, tag="eg", bufs=3, align_bytes=64)
-            for c, wb in enumerate(wbs):
-                bank = psum.tile([P, NT, P], F32, name="be", tag="bank")
-                for t in range(NT):
-                    for g in range(G):
-                        xl = N * g + P * t
-                        wl = D * g + P * wb
-                        nc.tensor.matmul_mx(
-                            out=bank[:, t, :],
-                            lhsT=x_cod[b][:, xl : xl + P].bitcast(FP8X4),
-                            lhsT_scale=x_scl[b][:, xl : xl + P],
-                            rhs=w_cod[1][:, wl : wl + P].bitcast(FP8X4),
-                            rhs_scale=w_scl[1][:, wl : wl + P],
-                            start=(g == 0),
-                            stop=(g == G - 1),
-                        )
-                evac(engs[c], eg[b][:, P * wb : P * wb + P, :], bank[:].rearrange("p t w -> p w t"))
-
-        def QE(b, h):
-            nc.vector.quantize_mx(
-                out=e_cod[b][:, 512 * h : 512 * h + 512].bitcast(FP8X4),
-                scales=e_scl[b][:, 512 * h : 512 * h + 512],
-                in_=eg[b][:, 512 * h : 512 * h + 512, :].rearrange("p c t -> p (c t)"),
-            )
-
-        an = {}
-        rr = {}
-
-        def RS(b):
-            rs = stage.tile([P, NT], F32, name="rs", tag="rs")
-            if RS_ACC:
-                for t in range(NT):
-                    junk = stage.tile([P, N], BF16, name="junk", tag="junk")
-                    nc.vector.tensor_scalar(
-                        out=junk[:], in0=a_raw[b][:, t, :], scalar1=1.0, scalar2=None,
-                        op0=ALU.mult, op1=ALU.add, accum_out=rs[:, t : t + 1],
+        def regroup_weight(i, g, lo, n, n_scalar):
+            tile = stage.tile([P, n, PACK], BF16, name="w_grouped", tag="w_grouped%d" % n, bufs=WAITING_COLUMNS // n, align_bytes=64)
+            w_grouped[(i, g, lo)] = tile
+            for copier, first, count in ((by_vector, 0, n - n_scalar), (by_scalar, n - n_scalar, n_scalar)):
+                if count:
+                    copier(
+                        tile[:, first : first + count, :].rearrange("p (c i) t -> p c t i", i=4),
+                        w_raw[i][:, g, :, lo + first : lo + first + count].rearrange("p t (c i) -> p c t i", i=4),
                     )
-            else:
-                nc.vector.tensor_reduce(out=rs[:], in_=a_raw[b][:], axis=AX.X, op=ALU.add)
-            zm = stage.tile([P, NT], F32, name="zm", tag="zm")
-            nc.vector.tensor_scalar(out=zm[:], in0=rs[:], scalar1=0.0, scalar2=None, op0=ALU.is_equal)
-            sf = stage.tile([P, NT], F32, name="sf", tag="sf")
-            nc.vector.tensor_tensor(out=sf[:], in0=rs[:], in1=zm[:], op=ALU.add)
-            rc = stage.tile([P, NT], F32, name="rc", tag="rc")
-            nc.vector.reciprocal(out=rc[:], in_=sf[:])
-            rr[b] = stage.tile([P, NT], F32, name="rr%d" % b, tag="rr")
-            nc.vector.tensor_tensor(out=rr[b][:], in0=rc[:], in1=zm[:], op=ALU.subtract)
 
-        def SC(b):
-            an[b] = stage.tile([P, NT, N], BF16, name="an%d" % b, tag="an")
-            for t in range(NT):
+        def quantise_weight(i, g, lo, n):
+            quantise(w_q[i], FEATS * g + lo, n, w_grouped[(i, g, lo)][:].rearrange("p c t -> p (c t)"))
+
+        e1_grouped = {}
+
+        def e1_blocks(b, blocks):
+            if b not in e1_grouped:
+                e1_grouped[b] = stage.tile([P, FEATS, PACK], BF16, name="e1_grouped%d" % b, tag="e1_grouped", bufs=3, align_bytes=64)
+            for block in blocks:
+                bank = psum.tile([P, NODE_TILES, P], F32, name="e1_bank", tag="bank")
+                for t in range(NODE_TILES):
+                    for g in range(PASSES):
+                        mx_pass(bank[:, t, :], x_q[b], NODES * g + P * t, w_q[W_E1], FEATS * g + P * block, P, g == 0, g == PASSES - 1)
+                by_scalar(e1_grouped[b][:, P * block : P * block + P, :], bank[:].rearrange("p t c -> p c t"))
+
+        def quantise_e1(b, half):
+            lo = BANK * half
+            quantise(e1_q[b], lo, BANK, e1_grouped[b][:, lo : lo + BANK, :].rearrange("p c t -> p (c t)"))
+
+        adj_n = {}
+        adj_grouped = {}
+
+        def normalise_adj(b):
+            rowsum = stage.tile([P, NODE_TILES], F32, name="rowsum", tag="rowsum")
+            for t in range(NODE_TILES):
+                unused = stage.tile([P, NODES], BF16, name="unused", tag="unused")
                 nc.vector.tensor_scalar(
-                    out=an[b][:, t, :], in0=a_raw[b][:, t, :], scalar1=rr[b][:, t : t + 1], scalar2=None, op0=ALU.mult
+                    out=unused[:], in0=adj_raw[b][:, t, :], scalar1=1.0, scalar2=None,
+                    op0=ALU.mult, op1=ALU.add, accum_out=rowsum[:, t : t + 1],
+                )
+            is_zero = stage.tile([P, NODE_TILES], F32, name="is_zero", tag="is_zero")
+            nc.vector.tensor_scalar(out=is_zero[:], in0=rowsum[:], scalar1=0.0, scalar2=None, op0=ALU.is_equal)
+            safe = stage.tile([P, NODE_TILES], F32, name="safe", tag="safe")
+            nc.vector.tensor_tensor(out=safe[:], in0=rowsum[:], in1=is_zero[:], op=ALU.add)
+            inverse = stage.tile([P, NODE_TILES], F32, name="inverse", tag="inverse")
+            nc.vector.reciprocal(out=inverse[:], in_=safe[:])
+            r = stage.tile([P, NODE_TILES], F32, name="r", tag="r")
+            nc.vector.tensor_tensor(out=r[:], in0=inverse[:], in1=is_zero[:], op=ALU.subtract)
+            adj_n[b] = stage.tile([P, NODE_TILES, NODES], BF16, name="adj_n%d" % b, tag="adj_n")
+            for t in range(NODE_TILES):
+                nc.vector.tensor_scalar(
+                    out=adj_n[b][:, t, :], in0=adj_raw[b][:, t, :], scalar1=r[:, t : t + 1], scalar2=None, op0=ALU.mult
                 )
 
-        def SCG(b):
-            an[b] = stage.tile([P, NT, N], BF16, name="an%d" % b, tag="an")
-            for t in range(NT):
-                nc.gpsimd.tensor_scalar(
-                    out=an[b][:, t, :], in0=a_raw[b][:, t, :], scalar1=rr[b][:, t : t + 1], scalar2=0.0,
-                    op0=ALU.mult, op1=ALU.add,
-                )
-
-        def RWG(i, g, h):
-            t = stage.tile([P, 512, 4], BF16, name="wg", tag="wg", bufs=4, align_bytes=64)
-            wg[(i, g, h)] = t
-            for k in range(4):
-                src = w_raw[i][:, g, :, 512 * h + 128 * k : 512 * h + 128 * k + 128]
-                nc.gpsimd.tensor_scalar(
-                    out=t[:, 128 * k : 128 * k + 128, :], in0=src.rearrange("p t c -> p c t"), scalar1=1.0, scalar2=0.0,
-                    op0=ALU.mult, op1=ALU.add,
-                )
-
-        ag = {}
-
-        def TA(b, engs):
-            ag[b] = stage.tile([P, N, 4], BF16, name="ag%d" % b, tag="ag", align_bytes=64)
-            for hi in range(2):
-                bank = psum.tile([P, NT, 256], BF16, name="ba", tag="bank")
-                for tj in range(NT):
-                    for ii in range(2):
+        def transpose_adj(b):
+            adj_grouped[b] = stage.tile([P, NODES, PACK], BF16, name="adj_grouped%d" % b, tag="adj_grouped", align_bytes=64)
+            filled = []
+            for half in range(2):
+                bank = psum.tile([P, NODE_TILES, 2 * P], BF16, name="adj_bank", tag="bank")
+                for t in range(NODE_TILES):
+                    for row_tile in range(2):
                         nc.tensor.transpose(
-                            bank[:, tj, 128 * ii : 128 * ii + 128],
-                            an[b][:, 2 * hi + ii, 128 * tj : 128 * tj + 128],
-                            ident_b[:],
+                            bank[:, t, P * row_tile : P * row_tile + P],
+                            adj_n[b][:, 2 * half + row_tile, P * t : P * t + P],
+                            ident_bf16[:],
                         )
-                evac(engs[hi], ag[b][:, 256 * hi : 256 * hi + 256, :], bank[:].rearrange("p t i -> p i t"))
+                filled.append(bank)
+            for half, bank in enumerate(filled):
+                by_scalar(adj_grouped[b][:, 2 * P * half : 2 * P * (half + 1), :], bank[:].rearrange("p t r -> p r t"))
 
-        def QA(b):
-            nc.vector.quantize_mx(
-                out=a_cod[b][:].bitcast(FP8X4), scales=a_scl[b][:], in_=ag[b][:].rearrange("p c t -> p (c t)")
-            )
+        def quantise_adj(b):
+            quantise(adj_q[b], 0, NODES, adj_grouped[b][:].rearrange("p r t -> p (r t)"))
 
-        res = {}
+        def leaky_relu_and_store(b, tile, result, lo, n):
+            part = result[:, lo : lo + n]
+            nc.vector.scalar_tensor_tensor(out=part, in0=part, scalar=SLOPE, in1=part, op0=ALU.mult, op1=ALU.max)
+            nc.sync.dma_start(out=out[b, P * tile : P * tile + P, lo : lo + n], in_=part)
 
-        def OP(b, ti, engs="SS"):
-            res[(b, ti)] = stage.tile([P, D], F32, name="res", tag="res", bufs=RES_BUFS)
-            for h in range(2):
-                bank = psum.tile([P, 512], F32, name="bo", tag="bank")
-                for g in range(G):
-                    xl = N * g + P * ti
-                    wl = D * g + 512 * h
-                    nc.tensor.matmul_mx(
-                        out=bank[:],
-                        lhsT=x_cod[b][:, xl : xl + P].bitcast(FP8X4),
-                        lhsT_scale=x_scl[b][:, xl : xl + P],
-                        rhs=w_cod[0][:, wl : wl + 512].bitcast(FP8X4),
-                        rhs_scale=w_scl[0][:, wl : wl + 512],
-                        start=(g == 0),
-                        stop=False,
-                    )
-                nc.tensor.matmul_mx(
-                    out=bank[:],
-                    lhsT=a_cod[b][:, P * ti : P * ti + P].bitcast(FP8X4),
-                    lhsT_scale=a_scl[b][:, P * ti : P * ti + P],
-                    rhs=e_cod[b][:, 512 * h : 512 * h + 512].bitcast(FP8X4),
-                    rhs_scale=e_scl[b][:, 512 * h : 512 * h + 512],
-                    start=False,
-                    stop=True,
-                )
-                evac(engs[h], res[(b, ti)][:, 512 * h : 512 * h + 512], bank[:])
+        def output_tiles(b, tiles, by_halves=False):
+            for tile in tiles:
+                result = stage.tile([P, FEATS], F32, name="result", tag="result", bufs=6)
+                for half in range(FEATS // BANK):
+                    lo = BANK * half
+                    bank = psum.tile([P, BANK], F32, name="out_bank", tag="bank")
+                    for g in range(PASSES):
+                        mx_pass(bank[:], x_q[b], NODES * g + P * tile, w_q[W_OUT], FEATS * g + lo, BANK, g == 0, False)
+                    mx_pass(bank[:], adj_q[b], P * tile, e1_q[b], lo, BANK, False, True)
+                    by_scalar(result[:, lo : lo + BANK], bank[:])
+                    if by_halves:
+                        leaky_relu_and_store(b, tile, result, lo, BANK)
+                if not by_halves:
+                    leaky_relu_and_store(b, tile, result, 0, FEATS)
 
-        def BS(b, ti, parts=1):
-            r = res[(b, ti)]
-            n = D // parts
-            for k in range(parts):
-                s = r[:, n * k : n * k + n]
-                nc.vector.scalar_tensor_tensor(out=s, in0=s, scalar=0.01, in1=s, op0=ALU.mult, op1=ALU.max)
-                nc.sync.dma_start(out=out[b, P * ti : P * ti + P, n * k : n * k + n], in_=s)
+        load_x(0, 2)
+        load_weight_columns(W_E1, 0, BANK)
+        load_weight_columns(W_E1, BANK, BANK)
+        load_x(1, 1)
+        load_x(2, 1)
+        load_adj(0)
+        load_x(3, 1)
+        load_adj(1)
+        load_weight_pass(W_OUT, 0)
+        load_weight_pass(W_OUT, 1)
+        load_adj(2)
+        load_adj(3)
 
-        def O(b, tis):
-            for ti in tis:
-                OP(b, ti)
-                BS(b, ti)
+        quarter = FEATS // 4
+        transpose_x(0, (by_scalar, by_vector, by_scalar, by_vector))
+        quantise_x(0)
+        for q in range(2):
+            for g in range(PASSES):
+                regroup_weight(W_E1, g, quarter * q, quarter, SCALAR_SHARE)
+        for q in range(2):
+            for g in range(PASSES):
+                quantise_weight(W_E1, g, quarter * q, quarter)
+            e1_blocks(0, (2 * q, 2 * q + 1))
+        for g in range(PASSES):
+            regroup_weight(W_E1, g, quarter * 2, quarter, 0)
+        for g in range(PASSES):
+            quantise_weight(W_E1, g, quarter * 2, quarter)
+        for g in range(PASSES):
+            regroup_weight(W_E1, g, quarter * 3, quarter, 0)
+        e1_blocks(0, (4, 5))
+        for g in range(PASSES):
+            quantise_weight(W_E1, g, quarter * 3, quarter)
 
-        banks = {}
+        transpose_x(1, (by_scalar, by_vector, by_scalar, by_vector))
+        quantise_e1(0, 0)
+        quantise_x(1)
+        e1_blocks(0, (6, 7))
+        transpose_x(2, (by_scalar,) * 4)
+        normalise_adj(0)
+        quantise_e1(0, 1)
+        e1_blocks(1, (0, 1, 2, 3))
+        quantise_x(2)
+        e1_blocks(1, (4, 5, 6, 7))
+        transpose_x(3, (by_scalar,) * 4)
+        normalise_adj(1)
+        quantise_x(3)
+        e1_blocks(2, (0, 1, 2, 3))
+        transpose_adj(0)
+        for g in range(PASSES):
+            for half in range(2):
+                regroup_weight(W_OUT, g, BANK * half, BANK, 0)
+            for half in range(2):
+                quantise_weight(W_OUT, g, BANK * half, BANK)
+            if g == 0:
+                quantise_adj(0)
+                e1_blocks(2, (4, 5, 6, 7))
+        e1_blocks(3, (0, 1, 2, 3))
+        transpose_adj(1)
+        e1_blocks(3, (4, 5, 6, 7))
+        quantise_e1(1, 0)
+        quantise_e1(1, 1)
+        quantise_adj(1)
+        normalise_adj(2)
 
-        def TXP(b, c):
-            if c == 0:
-                xg[b] = stage.tile([P, G * N * 4], BF16, name="xg%d" % b, tag="xg", align_bytes=64)
-            hn = c // 2
-            g = c % 2
-            xw = x_raw[b][:].bitcast(F32)
-            bank = psum.tile([P, 2, 256], F32, name="bx", tag="bank")
-            banks[("X", b, c)] = bank
-            for u in range(2):
-                for tt in range(2):
-                    col = 512 * (2 * hn + tt) + 256 * g + 128 * u
-                    nc.tensor.transpose(bank[:, u, 128 * tt : 128 * tt + 128], xw[:, col : col + 128], ident_f[:])
-
-        def EP(b, wb):
-            if b not in eg:
-                eg[b] = stage.tile([P, D, 4], BF16, name="eg%d" % b, tag="eg", bufs=3, align_bytes=64)
-            bank = psum.tile([P, NT, P], F32, name="be", tag="bank")
-            banks[("E", b, wb)] = bank
-            for t in range(NT):
-                for g in range(G):
-                    xl = N * g + P * t
-                    wl = D * g + P * wb
-                    nc.tensor.matmul_mx(
-                        out=bank[:, t, :],
-                        lhsT=x_cod[b][:, xl : xl + P].bitcast(FP8X4),
-                        lhsT_scale=x_scl[b][:, xl : xl + P],
-                        rhs=w_cod[1][:, wl : wl + P].bitcast(FP8X4),
-                        rhs_scale=w_scl[1][:, wl : wl + P],
-                        start=(g == 0),
-                        stop=(g == G - 1),
-                    )
-
-        def TAP(b, hi):
-            if hi == 0:
-                ag[b] = stage.tile([P, N, 4], BF16, name="ag%d" % b, tag="ag", align_bytes=64)
-            bank = psum.tile([P, NT, 256], BF16, name="ba", tag="bank")
-            banks[("A", b, hi)] = bank
-            for tj in range(NT):
-                for ii in range(2):
-                    nc.tensor.transpose(
-                        bank[:, tj, 128 * ii : 128 * ii + 128],
-                        an[b][:, 2 * hi + ii, 128 * tj : 128 * tj + 128],
-                        ident_b[:],
-                    )
-
-        def OPX(b, ti, h):
-            if h == 0:
-                res[(b, ti)] = stage.tile([P, D], F32, name="res", tag="res", bufs=RES_BUFS)
-            bank = psum.tile([P, 512], F32, name="bo", tag="bank")
-            banks[("O", b, 2 * ti + h)] = bank
-            for g in range(G):
-                xl = N * g + P * ti
-                wl = D * g + 512 * h
-                nc.tensor.matmul_mx(
-                    out=bank[:],
-                    lhsT=x_cod[b][:, xl : xl + P].bitcast(FP8X4),
-                    lhsT_scale=x_scl[b][:, xl : xl + P],
-                    rhs=w_cod[0][:, wl : wl + 512].bitcast(FP8X4),
-                    rhs_scale=w_scl[0][:, wl : wl + 512],
-                    start=(g == 0),
-                    stop=False,
-                )
-
-        def OPE(b, ti, h):
-            bank = banks[("O", b, 2 * ti + h)]
-            nc.tensor.matmul_mx(
-                out=bank[:],
-                lhsT=a_cod[b][:, P * ti : P * ti + P].bitcast(FP8X4),
-                lhsT_scale=a_scl[b][:, P * ti : P * ti + P],
-                rhs=e_cod[b][:, 512 * h : 512 * h + 512].bitcast(FP8X4),
-                rhs_scale=e_scl[b][:, 512 * h : 512 * h + 512],
-                start=False,
-                stop=True,
-            )
-
-        def EV(kind, b, c, eng):
-            bank = banks[(kind, b, c)]
-            if kind == "X":
-                dst = xg[b][:].bitcast(F32).rearrange("p (g n u) -> p g n u", g=G, u=2)
-                hn = c // 2
-                evac(eng, dst[:, c % 2, 256 * hn : 256 * hn + 256, :], bank[:].rearrange("p u n -> p n u"))
-            elif kind == "E":
-                evac(eng, eg[b][:, P * c : P * c + P, :], bank[:].rearrange("p t w -> p w t"))
-            elif kind == "A":
-                evac(eng, ag[b][:, 256 * c : 256 * c + 256, :], bank[:].rearrange("p t i -> p i t"))
+        output_tiles(0, (0, 1))
+        quantise_e1(2, 0)
+        quantise_e1(2, 1)
+        output_tiles(0, (2, 3))
+        normalise_adj(3)
+        for b in (1, 2):
+            transpose_adj(b + 1)
+            output_tiles(b, (0,))
+            quantise_adj(b + 1)
+            if b == 1:
+                output_tiles(b, (1,))
+                quantise_e1(3, 0)
+                output_tiles(b, (2, 3))
+                quantise_e1(3, 1)
             else:
-                h = c % 2
-                evac(eng, res[(b, c // 2)][:, 512 * h : 512 * h + 512], bank[:])
-
-        def RWp(i, g, h, eng, lo, n):
-            if (i, g, h) not in wg:
-                wg[(i, g, h)] = stage.tile([P, 512, 4], BF16, name="wg", tag="wg", bufs=4, align_bytes=64)
-            regroup(eng, wg[(i, g, h)][:, lo : lo + n, :], i, g, 512 * h + lo, n)
-
-        jobs = {
-            "TXP": TXP, "EP": EP, "TAP": TAP, "OPX": OPX, "OPE": OPE, "EV": EV, "RWp": RWp,
-            "LX": LX, "LA": LA, "LWC": LWC, "LWP": LWP, "TX": TX, "QX": QX, "RW": RW, "RW2": RW2, "QW": QW,
-            "E": E, "QE": QE, "RS": RS, "SC": SC, "TA": TA, "QA": QA, "O": O, "OP": OP, "BS": BS, "SCG": SCG, "RWG": RWG,
-        }
-        for step in PLAN:
-            jobs[step[0]](*step[1:])
+                output_tiles(b, (1, 2, 3))
+        output_tiles(3, (0, 1))
+        output_tiles(3, (2, 3), by_halves=True)

@@ -23,16 +23,13 @@ SLOPE = 0.01
 W_OUT = 0
 W_E1 = 1
 
-SCALAR_SHARE = 88
-
-WAITING_COLUMNS = 1024
+W_GROUPED_BUFS = {256: 3, 512: 2}
 
 FLOPS = 2 * (GRAPHS * NODES) * FEATS * FEATS * 2 + 2 * GRAPHS * NODES * NODES * FEATS
 
 
 def tile_graphnet_kernel(tc, X, adj, W_l, W_l1, out):
     nc = tc.nc
-    weights = [W_l, W_l1]
     with ExitStack() as ctx:
         ctx.enter_context(tc.manual_schedule())
         keep = ctx.enter_context(tc.tile_pool(name="keep", bufs=1))
@@ -41,12 +38,14 @@ def tile_graphnet_kernel(tc, X, adj, W_l, W_l1, out):
 
         ident_f32 = keep.tile([P, P], F32, name="ident_f32")
         make_identity(nc, ident_f32[:])
-        ident_bf16 = keep.tile([P, P], BF16, name="ident_bf16")
-        make_identity(nc, ident_bf16[:])
+        zeros = keep.tile([P, BANK], BF16, name="zeros")
+        nc.vector.memset(zeros[:], 0.0)
 
         x_raw = [keep.tile([P, NODE_TILES * FEATS], BF16, name="x_raw%d" % b, tag="x_raw", bufs=3) for b in range(GRAPHS)]
-        adj_raw = [keep.tile([P, NODE_TILES, NODES], BF16, name="adj_raw%d" % b) for b in range(GRAPHS)]
-        w_raw = {}
+        adj_raw = [keep.tile([P, NODE_TILES, NODES], BF16, name="adj_raw%d" % b, tag="adj_raw", bufs=3) for b in range(GRAPHS)]
+        quarter = FEATS // 4
+        w_e1_raw = [keep.tile([P, PASSES, PACK, quarter], BF16, name="w_e1_raw%d" % q) for q in range(4)]
+        w_out_raw = [keep.tile([P, PACK, FEATS], BF16, name="w_out_raw%d" % g) for g in range(PASSES)]
 
         def operand(name, columns):
             words = keep.tile([P, columns], U32, name=name + "_words", align_bytes=64)
@@ -80,30 +79,33 @@ def tile_graphnet_kernel(tc, X, adj, W_l, W_l1, out):
             nc.vector.tensor_copy(out=dst, in_=src)
 
         def load_x(b, pieces):
-            dst = x_raw[b][:].rearrange("p (t d) -> p t d", t=NODE_TILES)
-            src = X[b].rearrange("(t p) d -> p t d", p=P)
-            n = NODE_TILES // pieces
+            dst = x_raw[b][:].rearrange("p (u z) -> p u z", u=2)
+            src = X[b].rearrange("(u p e) d -> p u (e d)", p=P, e=2)
+            n = 2 // pieces
             for k in range(pieces):
                 nc.sync.dma_start(out=dst[:, n * k : n * k + n, :], in_=src[:, n * k : n * k + n, :])
 
         def load_adj(b):
-            nc.sync.dma_start(out=adj_raw[b][:], in_=adj[b].rearrange("(t p) j -> p t j", p=P))
+            nc.sync.dma_start(
+                out=adj_raw[b][:].rearrange("p (u e) j -> p u (e j)", e=2),
+                in_=adj[b].rearrange("(u p e) j -> p u (e j)", p=P, e=2),
+            )
 
-        def raw_weight(i):
-            if i not in w_raw:
-                w_raw[i] = keep.tile([P, PASSES, PACK, FEATS], BF16, name="w_raw%d" % i, tag="w_raw")
-            return w_raw[i]
-
-        def load_weight_columns(i, lo, n):
-            dst = raw_weight(i)[:].rearrange("p g (u e) c -> p (g u) e c", e=2)
-            src = weights[i].rearrange("(q p e) c -> p q e c", p=P, e=2)
+        def load_w_e1_quarter(q):
+            dst = w_e1_raw[q][:].rearrange("p g (u e) c -> p (g u) e c", e=2)
+            src = W_l1.rearrange("(q p e) c -> p q e c", p=P, e=2)
             for e in range(2):
-                nc.sync.dma_start(out=dst[:, :, e, lo : lo + n], in_=src[:, :, e, lo : lo + n])
+                nc.sync.dma_start(out=dst[:, :, e, :], in_=src[:, :, e, quarter * q : quarter * (q + 1)])
 
-        def load_weight_pass(i, g):
-            dst = raw_weight(i)[:, g].rearrange("p (u e) c -> p u e c", e=2)
-            rows = weights[i][P * PACK * g : P * PACK * (g + 1), :]
+        def load_w_out_pass(g):
+            dst = w_out_raw[g][:].rearrange("p (u e) c -> p u e c", e=2)
+            rows = W_l[P * PACK * g : P * PACK * (g + 1), :]
             nc.sync.dma_start(out=dst, in_=rows.rearrange("(u p e) c -> p u e c", p=P, e=2))
+
+        def warm_up(count):
+            for i in range(count):
+                bank = psum.tile([P, BANK], F32, name="warm_bank", tag="bank")
+                nc.tensor.matmul(out=bank[:], lhsT=zeros[:, 0:P], rhs=zeros[:], start=True, stop=True)
 
         x_grouped = {}
 
@@ -128,15 +130,14 @@ def tile_graphnet_kernel(tc, X, adj, W_l, W_l1, out):
 
         w_grouped = {}
 
-        def regroup_weight(i, g, lo, n, n_scalar):
-            tile = stage.tile([P, n, PACK], BF16, name="w_grouped", tag="w_grouped%d" % n, bufs=WAITING_COLUMNS // n, align_bytes=64)
+        def regroup_weight(i, g, lo, n, copier):
+            tile = stage.tile([P, n, PACK], BF16, name="w_grouped", tag="w_grouped%d" % n, bufs=W_GROUPED_BUFS[n], align_bytes=64)
             w_grouped[(i, g, lo)] = tile
-            for copier, first, count in ((by_vector, 0, n - n_scalar), (by_scalar, n - n_scalar, n_scalar)):
-                if count:
-                    copier(
-                        tile[:, first : first + count, :].rearrange("p (c i) t -> p c t i", i=4),
-                        w_raw[i][:, g, :, lo + first : lo + first + count].rearrange("p t (c i) -> p c t i", i=4),
-                    )
+            if i == W_E1:
+                raw = w_e1_raw[lo // quarter][:, g, :, :]
+            else:
+                raw = w_out_raw[g][:, :, lo : lo + n]
+            copier(tile[:].rearrange("p (c i) t -> p c t i", i=4), raw.rearrange("p t (c i) -> p c t i", i=4))
 
         def quantise_weight(i, g, lo, n):
             quantise(w_q[i], FEATS * g + lo, n, w_grouped[(i, g, lo)][:].rearrange("p c t -> p (c t)"))
@@ -160,43 +161,49 @@ def tile_graphnet_kernel(tc, X, adj, W_l, W_l1, out):
         adj_n = {}
         adj_grouped = {}
 
-        def normalise_adj(b):
-            rowsum = stage.tile([P, NODE_TILES], F32, name="rowsum", tag="rowsum")
+        rowsum = keep.tile([P, GRAPHS, NODE_TILES], F32, name="rowsum")
+        r = keep.tile([P, GRAPHS, NODE_TILES], F32, name="r")
+
+        def sum_adj_rows(b):
             for t in range(NODE_TILES):
                 unused = stage.tile([P, NODES], BF16, name="unused", tag="unused")
                 nc.vector.tensor_scalar(
                     out=unused[:], in0=adj_raw[b][:, t, :], scalar1=1.0, scalar2=None,
-                    op0=ALU.mult, op1=ALU.add, accum_out=rowsum[:, t : t + 1],
+                    op0=ALU.mult, op1=ALU.add, accum_out=rowsum[:, b, t : t + 1],
                 )
-            is_zero = stage.tile([P, NODE_TILES], F32, name="is_zero", tag="is_zero")
-            nc.vector.tensor_scalar(out=is_zero[:], in0=rowsum[:], scalar1=0.0, scalar2=None, op0=ALU.is_equal)
-            safe = stage.tile([P, NODE_TILES], F32, name="safe", tag="safe")
-            nc.vector.tensor_tensor(out=safe[:], in0=rowsum[:], in1=is_zero[:], op=ALU.add)
-            inverse = stage.tile([P, NODE_TILES], F32, name="inverse", tag="inverse")
+
+        def invert_row_sums(first):
+            sums = rowsum[:, first : first + 2, :].rearrange("p b t -> p (b t)")
+            safe = stage.tile([P, 2 * NODE_TILES], F32, name="safe", tag="safe")
+            nc.vector.scalar_tensor_tensor(out=safe[:], in0=sums, scalar=0.0, in1=sums, op0=ALU.is_equal, op1=ALU.add)
+            inverse = stage.tile([P, 2 * NODE_TILES], F32, name="inverse", tag="inverse")
             nc.vector.reciprocal(out=inverse[:], in_=safe[:])
-            r = stage.tile([P, NODE_TILES], F32, name="r", tag="r")
-            nc.vector.tensor_tensor(out=r[:], in0=inverse[:], in1=is_zero[:], op=ALU.subtract)
+            nc.vector.scalar_tensor_tensor(
+                out=r[:, first : first + 2, :].rearrange("p b t -> p (b t)"),
+                in0=sums, scalar=0.0, in1=inverse[:], op0=ALU.not_equal, op1=ALU.mult,
+            )
+
+        def scale_adj(b):
             adj_n[b] = stage.tile([P, NODE_TILES, NODES], BF16, name="adj_n%d" % b, tag="adj_n")
             for t in range(NODE_TILES):
                 nc.vector.tensor_scalar(
-                    out=adj_n[b][:, t, :], in0=adj_raw[b][:, t, :], scalar1=r[:, t : t + 1], scalar2=None, op0=ALU.mult
+                    out=adj_n[b][:, t, :], in0=adj_raw[b][:, t, :], scalar1=r[:, b, t : t + 1], scalar2=None, op0=ALU.mult
                 )
 
         def transpose_adj(b):
             adj_grouped[b] = stage.tile([P, NODES, PACK], BF16, name="adj_grouped%d" % b, tag="adj_grouped", align_bytes=64)
+            words = adj_n[b][:].rearrange("p t j -> p (t j)").bitcast(F32)
+            dst = adj_grouped[b][:].rearrange("p r t -> p (r t)").bitcast(F32).rearrange("p (r u) -> p r u", u=2)
             filled = []
             for half in range(2):
-                bank = psum.tile([P, NODE_TILES, 2 * P], BF16, name="adj_bank", tag="bank")
-                for t in range(NODE_TILES):
+                bank = psum.tile([P, 2, 2 * P], F32, name="adj_bank", tag="bank")
+                for u in range(2):
                     for row_tile in range(2):
-                        nc.tensor.transpose(
-                            bank[:, t, P * row_tile : P * row_tile + P],
-                            adj_n[b][:, 2 * half + row_tile, P * t : P * t + P],
-                            ident_bf16[:],
-                        )
+                        lo = (NODES // 2) * (2 * half + row_tile) + P * u
+                        nc.tensor.transpose(bank[:, u, P * row_tile : P * row_tile + P], words[:, lo : lo + P], ident_f32[:])
                 filled.append(bank)
             for half, bank in enumerate(filled):
-                by_scalar(adj_grouped[b][:, 2 * P * half : 2 * P * (half + 1), :], bank[:].rearrange("p t r -> p r t"))
+                by_scalar(dst[:, 2 * P * half : 2 * P * (half + 1), :], bank[:].rearrange("p u r -> p r u"))
 
         def quantise_adj(b):
             quantise(adj_q[b], 0, NODES, adj_grouped[b][:].rearrange("p r t -> p (r t)"))
@@ -204,7 +211,8 @@ def tile_graphnet_kernel(tc, X, adj, W_l, W_l1, out):
         def leaky_relu_and_store(b, tile, result, lo, n):
             part = result[:, lo : lo + n]
             nc.vector.scalar_tensor_tensor(out=part, in0=part, scalar=SLOPE, in1=part, op0=ALU.mult, op1=ALU.max)
-            nc.sync.dma_start(out=out[b, P * tile : P * tile + P, lo : lo + n], in_=part)
+            rows = out[b].rearrange("(u p e) d -> u e p d", p=P, e=2)[tile // 2, tile % 2]
+            nc.sync.dma_start(out=rows[:, lo : lo + n], in_=part)
 
         def output_tiles(b, tiles, by_halves=False):
             for tile in tiles:
@@ -222,84 +230,99 @@ def tile_graphnet_kernel(tc, X, adj, W_l, W_l1, out):
                     leaky_relu_and_store(b, tile, result, 0, FEATS)
 
         load_x(0, 2)
-        load_weight_columns(W_E1, 0, BANK)
-        load_weight_columns(W_E1, BANK, BANK)
+        load_w_e1_quarter(0)
         load_x(1, 1)
+        for q in range(1, 4):
+            load_w_e1_quarter(q)
         load_x(2, 1)
         load_adj(0)
-        load_x(3, 1)
         load_adj(1)
-        load_weight_pass(W_OUT, 0)
-        load_weight_pass(W_OUT, 1)
+        load_x(3, 1)
+        for g in range(PASSES):
+            load_w_out_pass(g)
         load_adj(2)
         load_adj(3)
 
-        quarter = FEATS // 4
-        transpose_x(0, (by_scalar, by_vector, by_scalar, by_vector))
-        quantise_x(0)
-        for q in range(2):
+        def regroup_e1_quarter(q, copiers):
             for g in range(PASSES):
-                regroup_weight(W_E1, g, quarter * q, quarter, SCALAR_SHARE)
-        for q in range(2):
+                regroup_weight(W_E1, g, quarter * q, quarter, copiers[g])
+
+        def quantise_e1_quarter(q):
             for g in range(PASSES):
                 quantise_weight(W_E1, g, quarter * q, quarter)
-            e1_blocks(0, (2 * q, 2 * q + 1))
-        for g in range(PASSES):
-            regroup_weight(W_E1, g, quarter * 2, quarter, 0)
-        for g in range(PASSES):
-            quantise_weight(W_E1, g, quarter * 2, quarter)
-        for g in range(PASSES):
-            regroup_weight(W_E1, g, quarter * 3, quarter, 0)
-        e1_blocks(0, (4, 5))
-        for g in range(PASSES):
-            quantise_weight(W_E1, g, quarter * 3, quarter)
 
-        transpose_x(1, (by_scalar, by_vector, by_scalar, by_vector))
-        quantise_e1(0, 0)
+        def regroup_w_out(g):
+            for half in range(2):
+                regroup_weight(W_OUT, g, BANK * half, BANK, by_vector)
+
+        def quantise_w_out(g):
+            for half in range(2):
+                quantise_weight(W_OUT, g, BANK * half, BANK)
+
+        warm_up(6)
+        transpose_x(0, (by_scalar, by_vector, by_scalar, by_vector))
+        warm_up(4)
+        quantise_x(0)
+        regroup_e1_quarter(0, (by_vector, by_scalar))
+        quantise_e1_quarter(0)
+        transpose_x(1, (by_scalar,) * 4)
+        e1_blocks(0, (0, 1))
+        regroup_e1_quarter(1, (by_vector, by_vector))
+        quantise_e1_quarter(1)
+        e1_blocks(0, (2, 3))
         quantise_x(1)
-        e1_blocks(0, (6, 7))
-        transpose_x(2, (by_scalar,) * 4)
-        normalise_adj(0)
-        quantise_e1(0, 1)
+        regroup_e1_quarter(2, (by_vector, by_vector))
+        quantise_e1_quarter(2)
         e1_blocks(1, (0, 1, 2, 3))
+        regroup_e1_quarter(3, (by_vector, by_vector))
+        quantise_e1_quarter(3)
+        e1_blocks(0, (4, 5))
+        transpose_x(2, (by_scalar, by_vector, by_scalar, by_vector))
+        e1_blocks(0, (6, 7))
+        sum_adj_rows(0)
         quantise_x(2)
         e1_blocks(1, (4, 5, 6, 7))
         transpose_x(3, (by_scalar,) * 4)
-        normalise_adj(1)
-        quantise_x(3)
+        quantise_e1(0, 0)
+        sum_adj_rows(1)
+        invert_row_sums(0)
         e1_blocks(2, (0, 1, 2, 3))
+        scale_adj(0)
+        scale_adj(1)
+        quantise_x(3)
+        regroup_w_out(0)
+        quantise_e1(0, 1)
+        e1_blocks(2, (4, 5, 6, 7))
+        quantise_w_out(0)
+        regroup_w_out(1)
+        quantise_w_out(1)
         transpose_adj(0)
-        for g in range(PASSES):
-            for half in range(2):
-                regroup_weight(W_OUT, g, BANK * half, BANK, 0)
-            for half in range(2):
-                quantise_weight(W_OUT, g, BANK * half, BANK)
-            if g == 0:
-                quantise_adj(0)
-                e1_blocks(2, (4, 5, 6, 7))
-        e1_blocks(3, (0, 1, 2, 3))
         transpose_adj(1)
+        e1_blocks(3, (0, 1, 2, 3))
+        quantise_adj(0)
         e1_blocks(3, (4, 5, 6, 7))
+
+        sum_adj_rows(2)
+        sum_adj_rows(3)
+        output_tiles(0, (0,))
+        invert_row_sums(2)
+        quantise_adj(1)
         quantise_e1(1, 0)
         quantise_e1(1, 1)
-        quantise_adj(1)
-        normalise_adj(2)
-
-        output_tiles(0, (0, 1))
+        output_tiles(0, (1, 2))
+        scale_adj(2)
+        scale_adj(3)
+        output_tiles(0, (3,))
+        output_tiles(1, (0, 1))
+        transpose_adj(2)
+        transpose_adj(3)
         quantise_e1(2, 0)
         quantise_e1(2, 1)
-        output_tiles(0, (2, 3))
-        normalise_adj(3)
-        for b in (1, 2):
-            transpose_adj(b + 1)
-            output_tiles(b, (0,))
-            quantise_adj(b + 1)
-            if b == 1:
-                output_tiles(b, (1,))
-                quantise_e1(3, 0)
-                output_tiles(b, (2, 3))
-                quantise_e1(3, 1)
-            else:
-                output_tiles(b, (1, 2, 3))
+        quantise_adj(2)
+        output_tiles(1, (2, 3))
+        quantise_adj(3)
+        quantise_e1(3, 0)
+        quantise_e1(3, 1)
+        output_tiles(2, (0, 1, 2, 3))
         output_tiles(3, (0, 1))
         output_tiles(3, (2, 3), by_halves=True)

@@ -72,6 +72,9 @@ def tile_graphnet_kernel(tc, X, adj, W_l, W_l1, out):
                 stop=stop,
             )
 
+        def x_column(g, tile):
+            return PASSES * 2 * P * (tile // 2) + 2 * P * g + P * (tile % 2)
+
         def by_scalar(dst, src):
             nc.scalar.copy(out=dst, in_=src)
 
@@ -109,24 +112,32 @@ def tile_graphnet_kernel(tc, X, adj, W_l, W_l1, out):
 
         x_grouped = {}
 
-        def transpose_x(b, copiers):
-            x_grouped[b] = stage.tile([P, PASSES * NODES * PACK], BF16, name="x_grouped%d" % b, tag="x_grouped", align_bytes=64)
+        def transpose_x_half(b, half, copiers):
+            if half == 0:
+                x_grouped[b] = stage.tile([P, PASSES * NODES * PACK], BF16, name="x_grouped%d" % b, tag="x_grouped", align_bytes=64)
             words = x_raw[b][:].bitcast(F32)
-            dst = x_grouped[b][:].bitcast(F32).rearrange("p (g n u) -> p g n u", g=PASSES, u=2)
-            filled = []
+            dst = x_grouped[b][:].bitcast(F32).rearrange("p (h g n u) -> p h g n u", h=2, g=PASSES, u=2)
+            banks = []
+            for g in range(PASSES):
+                bank = psum.tile([P, 2, 2 * P], F32, name="x_bank", tag="bank")
+                for u in range(2):
+                    for t in range(2):
+                        lo = (FEATS // 2) * (2 * half + t) + 2 * P * g + P * u
+                        nc.tensor.transpose(bank[:, u, P * t : P * t + P], words[:, lo : lo + P], ident_f32[:])
+                banks.append(bank)
+            for g in range(PASSES):
+                copiers[g](dst[:, half, g, :, :], banks[g][:].rearrange("p u n -> p n u"))
+
+        def transpose_x(b, copiers):
             for half in range(2):
-                for g in range(PASSES):
-                    bank = psum.tile([P, 2, 2 * P], F32, name="x_bank", tag="bank")
-                    for u in range(2):
-                        for t in range(2):
-                            lo = (FEATS // 2) * (2 * half + t) + 2 * P * g + P * u
-                            nc.tensor.transpose(bank[:, u, P * t : P * t + P], words[:, lo : lo + P], ident_f32[:])
-                    filled.append((bank, dst[:, g, 2 * P * half : 2 * P * (half + 1), :]))
-            for copier, (bank, where) in zip(copiers, filled):
-                copier(where, bank[:].rearrange("p u n -> p n u"))
+                transpose_x_half(b, half, copiers[2 * half : 2 * half + 2])
 
         def quantise_x(b):
             quantise(x_q[b], 0, PASSES * NODES, x_grouped[b][:])
+
+        def quantise_x_half(b, half):
+            n = PASSES * 2 * P
+            quantise(x_q[b], n * half, n, x_grouped[b][:, PACK * n * half : PACK * n * (half + 1)])
 
         w_grouped = {}
 
@@ -151,7 +162,7 @@ def tile_graphnet_kernel(tc, X, adj, W_l, W_l1, out):
                 bank = psum.tile([P, NODE_TILES, P], F32, name="e1_bank", tag="bank")
                 for t in range(NODE_TILES):
                     for g in range(PASSES):
-                        mx_pass(bank[:, t, :], x_q[b], NODES * g + P * t, w_q[W_E1], FEATS * g + P * block, P, g == 0, g == PASSES - 1)
+                        mx_pass(bank[:, t, :], x_q[b], x_column(g, t), w_q[W_E1], FEATS * g + P * block, P, g == 0, g == PASSES - 1)
                 by_scalar(e1_grouped[b][:, P * block : P * block + P, :], bank[:].rearrange("p t c -> p c t"))
 
         def quantise_e1(b, half):
@@ -208,30 +219,34 @@ def tile_graphnet_kernel(tc, X, adj, W_l, W_l1, out):
         def quantise_adj(b):
             quantise(adj_q[b], 0, NODES, adj_grouped[b][:].rearrange("p r t -> p (r t)"))
 
-        def leaky_relu_and_store(b, tile, result, lo, n):
-            part = result[:, lo : lo + n]
+        def leaky_relu_and_store(b, tile, lo, n, part):
             nc.vector.scalar_tensor_tensor(out=part, in0=part, scalar=SLOPE, in1=part, op0=ALU.mult, op1=ALU.max)
             rows = out[b].rearrange("(u p e) d -> u e p d", p=P, e=2)[tile // 2, tile % 2]
             nc.sync.dma_start(out=rows[:, lo : lo + n], in_=part)
 
-        def output_tiles(b, tiles, by_halves=False):
+        def output_part(b, tile, lo, n, part):
+            bank = psum.tile([P, BANK], F32, name="out_bank", tag="bank")
+            for g in range(PASSES):
+                mx_pass(bank[:, 0:n], x_q[b], x_column(g, tile), w_q[W_OUT], FEATS * g + lo, n, g == 0, False)
+            mx_pass(bank[:, 0:n], adj_q[b], P * tile, e1_q[b], lo, n, False, True)
+            by_scalar(part, bank[:, 0:n])
+
+        def output_tiles(b, tiles):
             for tile in tiles:
                 result = stage.tile([P, FEATS], F32, name="result", tag="result", bufs=6)
-                for half in range(FEATS // BANK):
-                    lo = BANK * half
-                    bank = psum.tile([P, BANK], F32, name="out_bank", tag="bank")
-                    for g in range(PASSES):
-                        mx_pass(bank[:], x_q[b], NODES * g + P * tile, w_q[W_OUT], FEATS * g + lo, BANK, g == 0, False)
-                    mx_pass(bank[:], adj_q[b], P * tile, e1_q[b], lo, BANK, False, True)
-                    by_scalar(result[:, lo : lo + BANK], bank[:])
-                    if by_halves:
-                        leaky_relu_and_store(b, tile, result, lo, BANK)
-                if not by_halves:
-                    leaky_relu_and_store(b, tile, result, 0, FEATS)
+                for lo in range(0, FEATS, BANK):
+                    output_part(b, tile, lo, BANK, result[:, lo : lo + BANK])
+                leaky_relu_and_store(b, tile, 0, FEATS, result[:])
+
+        def output_part_tiles(b, tiles, lo, n):
+            for tile in tiles:
+                result = stage.tile([P, n], F32, name="part_result", tag="result", bufs=6)
+                output_part(b, tile, lo, n, result[:])
+                leaky_relu_and_store(b, tile, lo, n, result[:])
 
         load_x(0, 2)
         load_w_e1_quarter(0)
-        load_x(1, 1)
+        load_x(1, 2)
         for q in range(1, 4):
             load_w_e1_quarter(q)
         load_x(2, 1)
@@ -260,20 +275,25 @@ def tile_graphnet_kernel(tc, X, adj, W_l, W_l1, out):
                 quantise_weight(W_OUT, g, BANK * half, BANK)
 
         warm_up(6)
-        transpose_x(0, (by_scalar, by_vector, by_scalar, by_vector))
-        warm_up(4)
-        quantise_x(0)
+        transpose_x_half(0, 0, (by_scalar, by_vector))
+        quantise_x_half(0, 0)
+        transpose_x_half(0, 1, (by_scalar, by_vector))
+        warm_up(2)
         regroup_e1_quarter(0, (by_vector, by_scalar))
+        quantise_x_half(0, 1)
         quantise_e1_quarter(0)
-        transpose_x(1, (by_scalar,) * 4)
+        transpose_x_half(1, 0, (by_vector, by_vector))
+        quantise_x_half(1, 0)
+        transpose_x_half(1, 1, (by_scalar, by_vector))
+        quantise_x_half(1, 1)
         e1_blocks(0, (0, 1))
         regroup_e1_quarter(1, (by_vector, by_vector))
         quantise_e1_quarter(1)
-        e1_blocks(0, (2, 3))
-        quantise_x(1)
+        e1_blocks(1, (0, 1))
         regroup_e1_quarter(2, (by_vector, by_vector))
         quantise_e1_quarter(2)
-        e1_blocks(1, (0, 1, 2, 3))
+        e1_blocks(0, (2, 3))
+        e1_blocks(1, (2, 3))
         regroup_e1_quarter(3, (by_vector, by_vector))
         quantise_e1_quarter(3)
         e1_blocks(0, (4, 5))
@@ -325,4 +345,7 @@ def tile_graphnet_kernel(tc, X, adj, W_l, W_l1, out):
         quantise_e1(3, 1)
         output_tiles(2, (0, 1, 2, 3))
         output_tiles(3, (0, 1))
-        output_tiles(3, (2, 3), by_halves=True)
+        output_part_tiles(3, (2,), 0, BANK)
+        output_part_tiles(3, (2,), BANK, BANK)
+        output_part_tiles(3, (3,), 0, BANK)
+        output_part_tiles(3, (3,), BANK, BANK)

@@ -105,10 +105,11 @@ def tile_graphnet_kernel(tc, X, adj, W_l, W_l1, out):
             rows = W_l[P * PACK * g : P * PACK * (g + 1), :]
             nc.sync.dma_start(out=dst, in_=rows.rearrange("(u p e) c -> p u e c", p=P, e=2))
 
-        def warm_up(count):
+        def warm_up(count, moving=None):
             for i in range(count):
                 bank = psum.tile([P, BANK], F32, name="warm_bank", tag="bank")
-                nc.tensor.matmul(out=bank[:], lhsT=zeros[:, 0:P], rhs=zeros[:], start=True, stop=True)
+                rhs = zeros[:] if moving is None else moving
+                nc.tensor.matmul(out=bank[:], lhsT=zeros[:, 0:P], rhs=rhs, start=True, stop=True)
 
         x_grouped = {}
 
@@ -279,11 +280,13 @@ def tile_graphnet_kernel(tc, X, adj, W_l, W_l1, out):
         quantise_x_half(0, 0)
         transpose_x_half(0, 1, (by_scalar, by_vector))
         warm_up(2)
+        warm_up(3, w_e1_raw[0][:, 0, 0:2, :].rearrange("p t c -> p (t c)"))
         regroup_e1_quarter(0, (by_vector, by_scalar))
         quantise_x_half(0, 1)
         quantise_e1_quarter(0)
         transpose_x_half(1, 0, (by_vector, by_vector))
         quantise_x_half(1, 0)
+        warm_up(2)
         transpose_x_half(1, 1, (by_scalar, by_vector))
         quantise_x_half(1, 1)
         e1_blocks(0, (0, 1))

@@ -184,15 +184,24 @@ def tile_graphnet_kernel(tc, X, adj, W_l, W_l1, out):
                     op0=ALU.mult, op1=ALU.add, accum_out=rowsum[:, b, t : t + 1],
                 )
 
-        def invert_row_sums(first):
-            sums = rowsum[:, first : first + 2, :].rearrange("p b t -> p (b t)")
-            safe = stage.tile([P, 2 * NODE_TILES], F32, name="safe", tag="safe")
-            nc.vector.scalar_tensor_tensor(out=safe[:], in0=sums, scalar=0.0, in1=sums, op0=ALU.is_equal, op1=ALU.add)
-            inverse = stage.tile([P, 2 * NODE_TILES], F32, name="inverse", tag="inverse")
-            nc.vector.reciprocal(out=inverse[:], in_=safe[:])
+        safe = {}
+        inverse = {}
+
+        def both(tile, first):
+            return tile[:, first : first + 2, :].rearrange("p b t -> p (b t)")
+
+        def invert_1(first):
+            sums = both(rowsum, first)
+            safe[first] = stage.tile([P, 2 * NODE_TILES], F32, name="safe", tag="safe")
+            nc.vector.scalar_tensor_tensor(out=safe[first][:], in0=sums, scalar=0.0, in1=sums, op0=ALU.is_equal, op1=ALU.add)
+
+        def invert_2(first):
+            inverse[first] = stage.tile([P, 2 * NODE_TILES], F32, name="inverse", tag="inverse")
+            nc.vector.reciprocal(out=inverse[first][:], in_=safe[first][:])
+
+        def invert_3(first):
             nc.vector.scalar_tensor_tensor(
-                out=r[:, first : first + 2, :].rearrange("p b t -> p (b t)"),
-                in0=sums, scalar=0.0, in1=inverse[:], op0=ALU.not_equal, op1=ALU.mult,
+                out=both(r, first), in0=both(rowsum, first), scalar=0.0, in1=inverse[first][:], op0=ALU.not_equal, op1=ALU.mult
             )
 
         def scale_adj(b):
@@ -278,16 +287,16 @@ def tile_graphnet_kernel(tc, X, adj, W_l, W_l1, out):
         warm_up(6)
         transpose_x_half(0, 0, (by_scalar, by_vector))
         quantise_x_half(0, 0)
-        transpose_x_half(0, 1, (by_scalar, by_vector))
+        transpose_x_half(0, 1, (by_scalar, by_scalar))
         warm_up(2)
         warm_up(3, w_e1_raw[0][:, 0, 0:2, :].rearrange("p t c -> p (t c)"))
         regroup_e1_quarter(0, (by_vector, by_scalar))
         quantise_x_half(0, 1)
         quantise_e1_quarter(0)
-        transpose_x_half(1, 0, (by_vector, by_vector))
+        transpose_x_half(1, 0, (by_scalar, by_scalar))
         quantise_x_half(1, 0)
         warm_up(2)
-        transpose_x_half(1, 1, (by_scalar, by_vector))
+        transpose_x_half(1, 1, (by_scalar, by_scalar))
         quantise_x_half(1, 1)
         e1_blocks(0, (0, 1))
         regroup_e1_quarter(1, (by_vector, by_vector))
@@ -306,31 +315,36 @@ def tile_graphnet_kernel(tc, X, adj, W_l, W_l1, out):
         quantise_x(2)
         e1_blocks(1, (4, 5, 6, 7))
         transpose_x(3, (by_scalar,) * 4)
-        quantise_e1(0, 0)
         sum_adj_rows(1)
-        invert_row_sums(0)
+        quantise_e1(0, 0)
+        invert_1(0)
+        quantise_e1(0, 1)
+        invert_2(0)
+        regroup_weight(W_OUT, 0, 0, BANK, by_vector)
+        invert_3(0)
+        regroup_weight(W_OUT, 0, BANK, BANK, by_vector)
         e1_blocks(2, (0, 1, 2, 3))
         scale_adj(0)
         scale_adj(1)
         quantise_x(3)
-        regroup_w_out(0)
-        quantise_e1(0, 1)
         e1_blocks(2, (4, 5, 6, 7))
         quantise_w_out(0)
         regroup_w_out(1)
-        quantise_w_out(1)
         transpose_adj(0)
         transpose_adj(1)
         e1_blocks(3, (0, 1, 2, 3))
         quantise_adj(0)
+        quantise_w_out(1)
         e1_blocks(3, (4, 5, 6, 7))
 
         sum_adj_rows(2)
         sum_adj_rows(3)
         output_tiles(0, (0,))
-        invert_row_sums(2)
+        invert_1(2)
         quantise_adj(1)
+        invert_2(2)
         quantise_e1(1, 0)
+        invert_3(2)
         quantise_e1(1, 1)
         output_tiles(0, (1, 2))
         scale_adj(2)

@@ -256,9 +256,10 @@ def tile_graphnet_kernel(tc, X, adj, W_l, W_l1, out):
 
         load_x(0, 2)
         load_w_e1_quarter(0)
+        load_w_e1_quarter(1)
         load_x(1, 2)
-        for q in range(1, 4):
-            load_w_e1_quarter(q)
+        load_w_e1_quarter(2)
+        load_w_e1_quarter(3)
         load_x(2, 1)
         load_adj(0)
         load_adj(1)
@@ -286,37 +287,37 @@ def tile_graphnet_kernel(tc, X, adj, W_l, W_l1, out):
 
         warm_up(6)
         transpose_x_half(0, 0, (by_scalar, by_vector))
-        quantise_x_half(0, 0)
         transpose_x_half(0, 1, (by_scalar, by_scalar))
+        quantise_x_half(0, 0)
         warm_up(2)
         warm_up(3, w_e1_raw[0][:, 0, 0:2, :].rearrange("p t c -> p (t c)"))
         regroup_e1_quarter(0, (by_vector, by_scalar))
         quantise_x_half(0, 1)
         quantise_e1_quarter(0)
-        transpose_x_half(1, 0, (by_scalar, by_scalar))
-        quantise_x_half(1, 0)
-        warm_up(2)
-        transpose_x_half(1, 1, (by_scalar, by_scalar))
-        quantise_x_half(1, 1)
         e1_blocks(0, (0, 1))
         regroup_e1_quarter(1, (by_vector, by_vector))
         quantise_e1_quarter(1)
+        transpose_x_half(1, 0, (by_scalar, by_vector))
+        transpose_x_half(1, 1, (by_scalar, by_vector))
+        quantise_x_half(1, 0)
+        e1_blocks(0, (2, 3))
+        quantise_x_half(1, 1)
         e1_blocks(1, (0, 1))
         regroup_e1_quarter(2, (by_vector, by_vector))
-        quantise_e1_quarter(2)
-        e1_blocks(0, (2, 3))
         e1_blocks(1, (2, 3))
-        regroup_e1_quarter(3, (by_vector, by_vector))
-        quantise_e1_quarter(3)
+        quantise_e1_quarter(2)
         e1_blocks(0, (4, 5))
+        regroup_e1_quarter(3, (by_vector, by_vector))
+        e1_blocks(1, (4, 5))
+        quantise_e1_quarter(3)
+        quantise_e1(0, 0)
+        sum_adj_rows(0)
         transpose_x(2, (by_scalar, by_vector, by_scalar, by_vector))
         e1_blocks(0, (6, 7))
-        sum_adj_rows(0)
         quantise_x(2)
-        e1_blocks(1, (4, 5, 6, 7))
-        transpose_x(3, (by_scalar,) * 4)
         sum_adj_rows(1)
-        quantise_e1(0, 0)
+        e1_blocks(1, (6, 7))
+        transpose_x(3, (by_scalar,) * 4)
         invert_1(0)
         quantise_e1(0, 1)
         invert_2(0)
@@ -329,9 +330,9 @@ def tile_graphnet_kernel(tc, X, adj, W_l, W_l1, out):
         quantise_x(3)
         e1_blocks(2, (4, 5, 6, 7))
         quantise_w_out(0)
-        regroup_w_out(1)
         transpose_adj(0)
         transpose_adj(1)
+        regroup_w_out(1)
         e1_blocks(3, (0, 1, 2, 3))
         quantise_adj(0)
         quantise_w_out(1)

@@ -241,12 +241,26 @@ def tile_graphnet_kernel(tc, X, adj, W_l, W_l1, out):
             mx_pass(bank[:, 0:n], adj_q[b], P * tile, e1_q[b], lo, n, False, True)
             by_scalar(part, bank[:, 0:n])
 
+        results = {}
+
         def output_tiles(b, tiles):
             for tile in tiles:
                 result = stage.tile([P, FEATS], F32, name="result", tag="result", bufs=6)
                 for lo in range(0, FEATS, BANK):
                     output_part(b, tile, lo, BANK, result[:, lo : lo + BANK])
-                leaky_relu_and_store(b, tile, 0, FEATS, result[:])
+                results[(b, tile)] = result
+
+        def output_tiles_half_by_half(b, tiles):
+            for tile in tiles:
+                result = stage.tile([P, FEATS], F32, name="result", tag="result", bufs=6)
+                results[(b, tile)] = result
+            for lo in range(0, FEATS, BANK):
+                for tile in tiles:
+                    output_part(b, tile, lo, BANK, results[(b, tile)][:, lo : lo + BANK])
+
+        def finish_tiles(b, tiles):
+            for tile in tiles:
+                leaky_relu_and_store(b, tile, 0, FEATS, results[(b, tile)][:])
 
         def output_part_tiles(b, tiles, lo, n):
             for tile in tiles:
@@ -298,7 +312,7 @@ def tile_graphnet_kernel(tc, X, adj, W_l, W_l1, out):
         regroup_e1_quarter(1, (by_vector, by_vector))
         quantise_e1_quarter(1)
         transpose_x_half(1, 0, (by_scalar, by_vector))
-        transpose_x_half(1, 1, (by_scalar, by_vector))
+        transpose_x_half(1, 1, (by_scalar, by_scalar))
         quantise_x_half(1, 0)
         e1_blocks(0, (2, 3))
         quantise_x_half(1, 1)
@@ -326,43 +340,57 @@ def tile_graphnet_kernel(tc, X, adj, W_l, W_l1, out):
         regroup_weight(W_OUT, 0, BANK, BANK, by_vector)
         e1_blocks(2, (0, 1, 2, 3))
         scale_adj(0)
-        scale_adj(1)
         quantise_x(3)
+        scale_adj(1)
         e1_blocks(2, (4, 5, 6, 7))
         quantise_w_out(0)
         transpose_adj(0)
         transpose_adj(1)
-        regroup_w_out(1)
+        regroup_weight(W_OUT, 1, 0, BANK, by_vector)
         e1_blocks(3, (0, 1, 2, 3))
         quantise_adj(0)
-        quantise_w_out(1)
+        quantise_weight(W_OUT, 1, 0, BANK)
         e1_blocks(3, (4, 5, 6, 7))
 
+        regroup_weight(W_OUT, 1, BANK, BANK, by_vector)
         sum_adj_rows(2)
+        quantise_weight(W_OUT, 1, BANK, BANK)
+        output_tiles_half_by_half(0, (0, 1, 2))
         sum_adj_rows(3)
-        output_tiles(0, (0,))
         invert_1(2)
         quantise_adj(1)
         invert_2(2)
         quantise_e1(1, 0)
         invert_3(2)
         quantise_e1(1, 1)
-        output_tiles(0, (1, 2))
+        output_tiles(0, (3,))
         scale_adj(2)
         scale_adj(3)
-        output_tiles(0, (3,))
-        output_tiles(1, (0, 1))
+        finish_tiles(0, (0, 1))
+        output_tiles(1, (0,))
+        quantise_e1(2, 0)
+        finish_tiles(0, (2,))
+        output_tiles(1, (1,))
         transpose_adj(2)
         transpose_adj(3)
-        quantise_e1(2, 0)
         quantise_e1(2, 1)
+        finish_tiles(0, (3,))
+        finish_tiles(1, (0,))
+        output_tiles(1, (2,))
         quantise_adj(2)
-        output_tiles(1, (2, 3))
+        finish_tiles(1, (1,))
+        output_tiles(1, (3,))
         quantise_adj(3)
+        finish_tiles(1, (2,))
         quantise_e1(3, 0)
+        finish_tiles(1, (3,))
         quantise_e1(3, 1)
-        output_tiles(2, (0, 1, 2, 3))
-        output_tiles(3, (0, 1))
+        for tile in range(NODE_TILES):
+            output_tiles(2, (tile,))
+            finish_tiles(2, (tile,))
+        for tile in range(2):
+            output_tiles(3, (tile,))
+            finish_tiles(3, (tile,))
         output_part_tiles(3, (2,), 0, BANK)
         output_part_tiles(3, (2,), BANK, BANK)
         output_part_tiles(3, (3,), 0, BANK)

@@ -45,7 +45,7 @@ def tile_graphnet_kernel(tc, X, adj, W_l, W_l1, out):
         adj_raw = [keep.tile([P, NODE_TILES, NODES], BF16, name="adj_raw%d" % b, tag="adj_raw", bufs=3) for b in range(GRAPHS)]
         quarter = FEATS // 4
         w_e1_raw = [keep.tile([P, PASSES, PACK, quarter], BF16, name="w_e1_raw%d" % q) for q in range(4)]
-        w_out_raw = [keep.tile([P, PACK, FEATS], BF16, name="w_out_raw%d" % g) for g in range(PASSES)]
+        w_out_raw = [keep.tile([P, PACK, FEATS], BF16, name="w_out_raw%d" % g, tag="x_raw", bufs=3) for g in range(PASSES)]
 
         def operand(name, columns):
             words = keep.tile([P, columns], U32, name=name + "_words", align_bytes=64)
@@ -245,14 +245,14 @@ def tile_graphnet_kernel(tc, X, adj, W_l, W_l1, out):
 
         def output_tiles(b, tiles):
             for tile in tiles:
-                result = stage.tile([P, FEATS], F32, name="result", tag="result", bufs=6)
+                result = stage.tile([P, FEATS], F32, name="result", tag="result", bufs=10)
                 for lo in range(0, FEATS, BANK):
                     output_part(b, tile, lo, BANK, result[:, lo : lo + BANK])
                 results[(b, tile)] = result
 
         def output_tiles_half_by_half(b, tiles):
             for tile in tiles:
-                result = stage.tile([P, FEATS], F32, name="result", tag="result", bufs=6)
+                result = stage.tile([P, FEATS], F32, name="result", tag="result", bufs=10)
                 results[(b, tile)] = result
             for lo in range(0, FEATS, BANK):
                 for tile in tiles:
@@ -264,7 +264,7 @@ def tile_graphnet_kernel(tc, X, adj, W_l, W_l1, out):
 
         def output_part_tiles(b, tiles, lo, n):
             for tile in tiles:
-                result = stage.tile([P, n], F32, name="part_result", tag="result", bufs=6)
+                result = stage.tile([P, n], F32, name="part_result", tag="result", bufs=10)
                 output_part(b, tile, lo, n, result[:])
                 leaky_relu_and_store(b, tile, lo, n, result[:])
 
@@ -335,14 +335,13 @@ def tile_graphnet_kernel(tc, X, adj, W_l, W_l1, out):
         invert_1(0)
         quantise_e1(0, 1)
         invert_2(0)
-        regroup_weight(W_OUT, 0, 0, BANK, by_vector)
         invert_3(0)
-        regroup_weight(W_OUT, 0, BANK, BANK, by_vector)
         e1_blocks(2, (0, 1, 2, 3))
         scale_adj(0)
-        quantise_x(3)
         scale_adj(1)
+        quantise_x(3)
         e1_blocks(2, (4, 5, 6, 7))
+        regroup_w_out(0)
         quantise_w_out(0)
         transpose_adj(0)
         transpose_adj(1)
@@ -353,28 +352,28 @@ def tile_graphnet_kernel(tc, X, adj, W_l, W_l1, out):
         e1_blocks(3, (4, 5, 6, 7))
 
         regroup_weight(W_OUT, 1, BANK, BANK, by_vector)
-        sum_adj_rows(2)
+        quantise_adj(1)
         quantise_weight(W_OUT, 1, BANK, BANK)
-        output_tiles_half_by_half(0, (0, 1, 2))
+        output_tiles_half_by_half(0, (0, 1, 2, 3))
+        sum_adj_rows(2)
         sum_adj_rows(3)
         invert_1(2)
-        quantise_adj(1)
-        invert_2(2)
         quantise_e1(1, 0)
-        invert_3(2)
+        invert_2(2)
         quantise_e1(1, 1)
-        output_tiles(0, (3,))
+        invert_3(2)
+        finish_tiles(0, (0,))
+        finish_tiles(0, (1,))
         scale_adj(2)
         scale_adj(3)
-        finish_tiles(0, (0, 1))
+        finish_tiles(0, (2,))
         output_tiles(1, (0,))
         quantise_e1(2, 0)
-        finish_tiles(0, (2,))
+        finish_tiles(0, (3,))
         output_tiles(1, (1,))
         transpose_adj(2)
         transpose_adj(3)
         quantise_e1(2, 1)
-        finish_tiles(0, (3,))
         finish_tiles(1, (0,))
         output_tiles(1, (2,))
         quantise_adj(2)

@@ -44,7 +44,7 @@ def tile_graphnet_kernel(tc, X, adj, W_l, W_l1, out):
         x_raw = [keep.tile([P, NODE_TILES * FEATS], BF16, name="x_raw%d" % b, tag="x_raw", bufs=3) for b in range(GRAPHS)]
         adj_raw = [keep.tile([P, NODE_TILES, NODES], BF16, name="adj_raw%d" % b, tag="adj_raw", bufs=3) for b in range(GRAPHS)]
         quarter = FEATS // 4
-        w_e1_raw = [keep.tile([P, PASSES, PACK, quarter], BF16, name="w_e1_raw%d" % q) for q in range(4)]
+        w_e1_raw = [[keep.tile([P, PACK, BANK], BF16, name="w_e1_raw%d%d" % (c, g)) for g in range(PASSES)] for c in range(2)]
         w_out_raw = [keep.tile([P, PACK, FEATS], BF16, name="w_out_raw%d" % g, tag="x_raw", bufs=3) for g in range(PASSES)]
 
         def operand(name, columns):
@@ -94,11 +94,10 @@ def tile_graphnet_kernel(tc, X, adj, W_l, W_l1, out):
                 in_=adj[b].rearrange("(u p e) j -> p u (e j)", p=P, e=2),
             )
 
-        def load_w_e1_quarter(q):
-            dst = w_e1_raw[q][:].rearrange("p g (u e) c -> p (g u) e c", e=2)
-            src = W_l1.rearrange("(q p e) c -> p q e c", p=P, e=2)
-            for e in range(2):
-                nc.sync.dma_start(out=dst[:, :, e, :], in_=src[:, :, e, quarter * q : quarter * (q + 1)])
+        def load_w_e1(c, g):
+            for u in range(2):
+                rows = W_l1[2 * P * (2 * g + u) : 2 * P * (2 * g + u + 1), BANK * c : BANK * (c + 1)]
+                nc.sync.dma_start(out=w_e1_raw[c][g][:, 2 * u : 2 * u + 2, :], in_=rows.rearrange("(p e) c -> p e c", e=2))
 
         def load_w_out_pass(g):
             dst = w_out_raw[g][:].rearrange("p (u e) c -> p u e c", e=2)
@@ -146,7 +145,7 @@ def tile_graphnet_kernel(tc, X, adj, W_l, W_l1, out):
             tile = stage.tile([P, n, PACK], BF16, name="w_grouped", tag="w_grouped%d" % n, bufs=W_GROUPED_BUFS[n], align_bytes=64)
             w_grouped[(i, g, lo)] = tile
             if i == W_E1:
-                raw = w_e1_raw[lo // quarter][:, g, :, :]
+                raw = w_e1_raw[lo // BANK][g][:, :, lo % BANK : lo % BANK + n]
             else:
                 raw = w_out_raw[g][:, :, lo : lo + n]
             copier(tile[:].rearrange("p (c i) t -> p c t i", i=4), raw.rearrange("p t (c i) -> p c t i", i=4))
@@ -269,11 +268,11 @@ def tile_graphnet_kernel(tc, X, adj, W_l, W_l1, out):
                 leaky_relu_and_store(b, tile, lo, n, result[:])
 
         load_x(0, 2)
-        load_w_e1_quarter(0)
-        load_w_e1_quarter(1)
+        for g in range(PASSES):
+            load_w_e1(0, g)
         load_x(1, 2)
-        load_w_e1_quarter(2)
-        load_w_e1_quarter(3)
+        for g in range(PASSES):
+            load_w_e1(1, g)
         load_x(2, 1)
         load_adj(0)
         load_adj(1)
@@ -304,16 +303,21 @@ def tile_graphnet_kernel(tc, X, adj, W_l, W_l1, out):
         transpose_x_half(0, 1, (by_scalar, by_scalar))
         quantise_x_half(0, 0)
         warm_up(2)
-        warm_up(3, w_e1_raw[0][:, 0, 0:2, :].rearrange("p t c -> p (t c)"))
-        regroup_e1_quarter(0, (by_vector, by_scalar))
+        warm_up(4, w_e1_raw[0][0][:, 0, :])
+        regroup_weight(W_E1, 0, 0, quarter, by_vector)
         quantise_x_half(0, 1)
-        quantise_e1_quarter(0)
+        quantise_weight(W_E1, 0, 0, quarter)
+        regroup_weight(W_E1, 0, quarter, quarter, by_scalar)
+        regroup_weight(W_E1, 1, 0, quarter, by_vector)
+        quantise_weight(W_E1, 0, quarter, quarter)
+        quantise_weight(W_E1, 1, 0, quarter)
+        warm_up(4, w_e1_raw[0][1][:, 0, :])
+        transpose_x_half(1, 0, (by_scalar, by_scalar))
         e1_blocks(0, (0, 1))
-        regroup_e1_quarter(1, (by_vector, by_vector))
-        quantise_e1_quarter(1)
-        transpose_x_half(1, 0, (by_scalar, by_vector))
-        transpose_x_half(1, 1, (by_scalar, by_scalar))
+        regroup_weight(W_E1, 1, quarter, quarter, by_vector)
         quantise_x_half(1, 0)
+        quantise_weight(W_E1, 1, quarter, quarter)
+        transpose_x_half(1, 1, (by_scalar, by_vector))
         e1_blocks(0, (2, 3))
         quantise_x_half(1, 1)
         e1_blocks(1, (0, 1))

@@ -330,15 +330,16 @@ def tile_graphnet_kernel(tc, X, adj, W_l, W_l1, out):
         quantise_e1_quarter(3)
         quantise_e1(0, 0)
         sum_adj_rows(0)
-        transpose_x(2, (by_scalar, by_vector, by_scalar, by_vector))
+        transpose_x(2, (by_scalar, by_vector, by_scalar, by_scalar))
+        sum_adj_rows(1)
         e1_blocks(0, (6, 7))
         quantise_x(2)
-        sum_adj_rows(1)
         e1_blocks(1, (6, 7))
         transpose_x(3, (by_scalar,) * 4)
         invert_1(0)
         quantise_e1(0, 1)
         invert_2(0)
+        quantise_e1(1, 0)
         invert_3(0)
         e1_blocks(2, (0, 1, 2, 3))
         scale_adj(0)
@@ -362,7 +363,6 @@ def tile_graphnet_kernel(tc, X, adj, W_l, W_l1, out):
         sum_adj_rows(2)
         sum_adj_rows(3)
         invert_1(2)
-        quantise_e1(1, 0)
         invert_2(2)
         quantise_e1(1, 1)
         invert_3(2)

@@ -23,7 +23,7 @@ SLOPE = 0.01
 W_OUT = 0
 W_E1 = 1
 
-W_GROUPED_BUFS = {256: 3, 512: 2}
+W_GROUPED_BUFS = {256: 3, 512: 2, 1024: 1}
 
 FLOPS = 2 * (GRAPHS * NODES) * FEATS * FEATS * 2 + 2 * GRAPHS * NODES * NODES * FEATS
 
@@ -228,10 +228,16 @@ def tile_graphnet_kernel(tc, X, adj, W_l, W_l1, out):
         def quantise_adj(b):
             quantise(adj_q[b], 0, NODES, adj_grouped[b][:].rearrange("p r t -> p (r t)"))
 
-        def leaky_relu_and_store(b, tile, lo, n, part):
+        def leaky_relu(part):
             nc.vector.scalar_tensor_tensor(out=part, in0=part, scalar=SLOPE, in1=part, op0=ALU.mult, op1=ALU.max)
+
+        def store(b, tile, lo, n, part):
             rows = out[b].rearrange("(u p e) d -> u e p d", p=P, e=2)[tile // 2, tile % 2]
             nc.sync.dma_start(out=rows[:, lo : lo + n], in_=part)
+
+        def leaky_relu_and_store(b, tile, lo, n, part):
+            leaky_relu(part)
+            store(b, tile, lo, n, part)
 
         def output_part(b, tile, lo, n, part):
             bank = psum.tile([P, BANK], F32, name="out_bank", tag="bank")
@@ -244,14 +250,14 @@ def tile_graphnet_kernel(tc, X, adj, W_l, W_l1, out):
 
         def output_tiles(b, tiles):
             for tile in tiles:
-                result = stage.tile([P, FEATS], F32, name="result", tag="result", bufs=10)
+                result = stage.tile([P, FEATS], F32, name="result", tag="result", bufs=8)
                 for lo in range(0, FEATS, BANK):
                     output_part(b, tile, lo, BANK, result[:, lo : lo + BANK])
                 results[(b, tile)] = result
 
         def output_tiles_half_by_half(b, tiles):
             for tile in tiles:
-                result = stage.tile([P, FEATS], F32, name="result", tag="result", bufs=10)
+                result = stage.tile([P, FEATS], F32, name="result", tag="result", bufs=8)
                 results[(b, tile)] = result
             for lo in range(0, FEATS, BANK):
                 for tile in tiles:
@@ -261,9 +267,18 @@ def tile_graphnet_kernel(tc, X, adj, W_l, W_l1, out):
             for tile in tiles:
                 leaky_relu_and_store(b, tile, 0, FEATS, results[(b, tile)][:])
 
+        def output_tiles_by_halves(b, tiles):
+            for tile in tiles:
+                result = stage.tile([P, FEATS], F32, name="result", tag="result", bufs=8)
+                for lo in range(0, FEATS, BANK):
+                    part = result[:, lo : lo + BANK]
+                    output_part(b, tile, lo, BANK, part)
+                    leaky_relu(part)
+                store(b, tile, 0, FEATS, result[:])
+
         def output_part_tiles(b, tiles, lo, n):
             for tile in tiles:
-                result = stage.tile([P, n], F32, name="part_result", tag="result", bufs=10)
+                result = stage.tile([P, n], F32, name="part_result", tag="result", bufs=8)
                 output_part(b, tile, lo, n, result[:])
                 leaky_relu_and_store(b, tile, lo, n, result[:])
 
@@ -274,9 +289,9 @@ def tile_graphnet_kernel(tc, X, adj, W_l, W_l1, out):
         for g in range(PASSES):
             load_w_e1(1, g)
         load_x(2, 1)
+        load_x(3, 1)
         load_adj(0)
         load_adj(1)
-        load_x(3, 1)
         for g in range(PASSES):
             load_w_out_pass(g)
         load_adj(2)
@@ -291,12 +306,13 @@ def tile_graphnet_kernel(tc, X, adj, W_l, W_l1, out):
                 quantise_weight(W_E1, g, quarter * q, quarter)
 
         def regroup_w_out(g):
-            for half in range(2):
-                regroup_weight(W_OUT, g, BANK * half, BANK, by_vector)
+            regroup_weight(W_OUT, g, 0, FEATS, by_vector)
 
         def quantise_w_out(g):
-            for half in range(2):
-                quantise_weight(W_OUT, g, BANK * half, BANK)
+            quantise_weight(W_OUT, g, 0, FEATS)
+
+        def quantise_e1_whole(b):
+            quantise(e1_q[b], 0, FEATS, e1_grouped[b][:].rearrange("p c t -> p (c t)"))
 
         warm_up(6)
         transpose_x_half(0, 0, (by_scalar, by_vector))
@@ -329,22 +345,22 @@ def tile_graphnet_kernel(tc, X, adj, W_l, W_l1, out):
         e1_blocks(1, (4, 5))
         quantise_e1_quarter(3)
         quantise_e1(0, 0)
-        sum_adj_rows(0)
+        quantise_e1(1, 0)
         transpose_x(2, (by_scalar, by_vector, by_scalar, by_scalar))
-        sum_adj_rows(1)
+        sum_adj_rows(0)
+        transpose_x(3, (by_scalar,) * 4)
         e1_blocks(0, (6, 7))
         quantise_x(2)
         e1_blocks(1, (6, 7))
-        transpose_x(3, (by_scalar,) * 4)
+        sum_adj_rows(1)
+        quantise_x(3)
         invert_1(0)
         quantise_e1(0, 1)
         invert_2(0)
-        quantise_e1(1, 0)
         invert_3(0)
         e1_blocks(2, (0, 1, 2, 3))
         scale_adj(0)
         scale_adj(1)
-        quantise_x(3)
         e1_blocks(2, (4, 5, 6, 7))
         regroup_w_out(0)
         quantise_w_out(0)
@@ -372,12 +388,11 @@ def tile_graphnet_kernel(tc, X, adj, W_l, W_l1, out):
         scale_adj(3)
         finish_tiles(0, (2,))
         output_tiles(1, (0,))
-        quantise_e1(2, 0)
         finish_tiles(0, (3,))
         output_tiles(1, (1,))
         transpose_adj(2)
         transpose_adj(3)
-        quantise_e1(2, 1)
+        quantise_e1_whole(2)
         finish_tiles(1, (0,))
         output_tiles(1, (2,))
         quantise_adj(2)
@@ -385,15 +400,12 @@ def tile_graphnet_kernel(tc, X, adj, W_l, W_l1, out):
         output_tiles(1, (3,))
         quantise_adj(3)
         finish_tiles(1, (2,))
-        quantise_e1(3, 0)
         finish_tiles(1, (3,))
-        quantise_e1(3, 1)
+        quantise_e1_whole(3)
         for tile in range(NODE_TILES):
             output_tiles(2, (tile,))
             finish_tiles(2, (tile,))
-        for tile in range(2):
-            output_tiles(3, (tile,))
-            finish_tiles(3, (tile,))
+        output_tiles_by_halves(3, (0, 1))
         output_part_tiles(3, (2,), 0, BANK)
         output_part_tiles(3, (2,), BANK, BANK)
         output_part_tiles(3, (3,), 0, BANK)

@@ -165,6 +165,18 @@ def tile_graphnet_kernel(tc, X, adj, W_l, W_l1, out):
                         mx_pass(bank[:, t, :], x_q[b], x_column(g, t), w_q[W_E1], FEATS * g + P * block, P, g == 0, g == PASSES - 1)
                 by_scalar(e1_grouped[b][:, P * block : P * block + P, :], bank[:].rearrange("p t c -> p c t"))
 
+        def e1_blocks_wide(b, blocks):
+            if b not in e1_grouped:
+                e1_grouped[b] = stage.tile([P, FEATS, PACK], BF16, name="e1_grouped%d" % b, tag="e1_grouped", bufs=3, align_bytes=64)
+            for block in blocks[::2]:
+                lo = P * block
+                for half in range(2):
+                    bank = psum.tile([P, 2, 2 * P], F32, name="e1_wide_bank", tag="bank")
+                    for i in range(2):
+                        for g in range(PASSES):
+                            mx_pass(bank[:, i, :], x_q[b], x_column(g, 2 * half + i), w_q[W_E1], FEATS * g + lo, 2 * P, g == 0, g == PASSES - 1)
+                    by_scalar(e1_grouped[b][:, lo : lo + 2 * P, 2 * half : 2 * half + 2], bank[:].rearrange("p t c -> p c t"))
+
         def quantise_e1(b, half):
             lo = BANK * half
             quantise(e1_q[b], lo, BANK, e1_grouped[b][:, lo : lo + BANK, :].rearrange("p c t -> p (c t)"))
@@ -314,7 +326,7 @@ def tile_graphnet_kernel(tc, X, adj, W_l, W_l1, out):
         def quantise_e1_whole(b):
             quantise(e1_q[b], 0, FEATS, e1_grouped[b][:].rearrange("p c t -> p (c t)"))
 
-        warm_up(6)
+        warm_up(5)
         transpose_x_half(0, 0, (by_scalar, by_vector))
         transpose_x_half(0, 1, (by_scalar, by_scalar))
         quantise_x_half(0, 0)
@@ -353,21 +365,22 @@ def tile_graphnet_kernel(tc, X, adj, W_l, W_l1, out):
         quantise_x(2)
         e1_blocks(1, (6, 7))
         sum_adj_rows(1)
-        quantise_x(3)
+        quantise_x_half(3, 0)
         invert_1(0)
-        quantise_e1(0, 1)
+        quantise_x_half(3, 1)
         invert_2(0)
+        quantise_e1(0, 1)
         invert_3(0)
         e1_blocks(2, (0, 1, 2, 3))
         scale_adj(0)
         scale_adj(1)
         e1_blocks(2, (4, 5, 6, 7))
         regroup_w_out(0)
+        regroup_weight(W_OUT, 1, 0, BANK, by_vector)
         quantise_w_out(0)
         transpose_adj(0)
         transpose_adj(1)
-        regroup_weight(W_OUT, 1, 0, BANK, by_vector)
-        e1_blocks(3, (0, 1, 2, 3))
+        e1_blocks_wide(3, (0, 1, 2, 3))
         quantise_adj(0)
         quantise_weight(W_OUT, 1, 0, BANK)
         e1_blocks(3, (4, 5, 6, 7))
@@ -378,11 +391,12 @@ def tile_graphnet_kernel(tc, X, adj, W_l, W_l1, out):
         output_tiles_half_by_half(0, (0, 1, 2, 3))
         sum_adj_rows(2)
         sum_adj_rows(3)
-        invert_1(2)
-        invert_2(2)
         quantise_e1(1, 1)
-        invert_3(2)
+        invert_1(2)
+        quantise_e1_whole(2)
+        invert_2(2)
         finish_tiles(0, (0,))
+        invert_3(2)
         finish_tiles(0, (1,))
         scale_adj(2)
         scale_adj(3)
@@ -392,7 +406,6 @@ def tile_graphnet_kernel(tc, X, adj, W_l, W_l1, out):
         output_tiles(1, (1,))
         transpose_adj(2)
         transpose_adj(3)
-        quantise_e1_whole(2)
         finish_tiles(1, (0,))
         output_tiles(1, (2,))
         quantise_adj(2)

from contextlib import ExitStack

import concourse.mybir as mybir
from concourse.masks import make_identity

F32 = mybir.dt.float32
BF16 = mybir.dt.bfloat16
U32 = mybir.dt.uint32
U8 = mybir.dt.uint8
FP8X4 = mybir.dt.float8_e4m3fn_x4
ALU = mybir.AluOpType

P = 128
PACK = 4
GRAPHS = 4
NODES = 512
FEATS = 1024
NODE_TILES = NODES // P
PASSES = FEATS // (P * PACK)
BANK = 512
SLOPE = 0.01

W_OUT = 0
W_E1 = 1

W_GROUPED_BUFS = {256: 3, 512: 2, 1024: 1}

FLOPS = 2 * (GRAPHS * NODES) * FEATS * FEATS * 2 + 2 * GRAPHS * NODES * NODES * FEATS


def tile_graphnet_kernel(tc, X, adj, W_l, W_l1, out):
    nc = tc.nc
    with ExitStack() as ctx:
        ctx.enter_context(tc.manual_schedule())
        keep = ctx.enter_context(tc.tile_pool(name="keep", bufs=1))
        stage = ctx.enter_context(tc.tile_pool(name="stage", bufs=2))
        psum = ctx.enter_context(tc.psum_pool(name="psum", bufs=8))

        ident_f32 = keep.tile([P, P], F32, name="ident_f32")
        make_identity(nc, ident_f32[:])
        zeros = keep.tile([P, BANK], BF16, name="zeros")
        nc.vector.memset(zeros[:], 0.0)

        x_raw = [keep.tile([P, NODE_TILES * FEATS], BF16, name="x_raw%d" % b, tag="x_raw", bufs=3) for b in range(GRAPHS)]
        adj_raw = [keep.tile([P, NODE_TILES, NODES], BF16, name="adj_raw%d" % b, tag="adj_raw", bufs=3) for b in range(GRAPHS)]
        quarter = FEATS // 4
        w_e1_raw = [[keep.tile([P, PACK, BANK], BF16, name="w_e1_raw%d%d" % (c, g)) for g in range(PASSES)] for c in range(2)]
        w_out_raw = [keep.tile([P, PACK, FEATS], BF16, name="w_out_raw%d" % g, tag="x_raw", bufs=3) for g in range(PASSES)]

        def operand(name, columns):
            words = keep.tile([P, columns], U32, name=name + "_words", align_bytes=64)
            plane = keep.tile([P, columns], U8, name=name + "_plane", align_bytes=64)
            return words, plane

        x_q = [operand("x%d" % b, PASSES * NODES) for b in range(GRAPHS)]
        w_q = [operand("w%d" % i, PASSES * FEATS) for i in range(2)]
        adj_q = [operand("adj%d" % b, NODES) for b in range(GRAPHS)]
        e1_q = [operand("e1_%d" % b, FEATS) for b in range(GRAPHS)]

        def quantise(operand_q, lo, n, grouped):
            words, plane = operand_q
            nc.vector.quantize_mx(out=words[:, lo : lo + n].bitcast(FP8X4), scales=plane[:, lo : lo + n], in_=grouped)

        def mx_pass(acc, lhs_q, lhs_lo, rhs_q, rhs_lo, n, start, stop):
            nc.tensor.matmul_mx(
                out=acc,
                lhsT=lhs_q[0][:, lhs_lo : lhs_lo + P].bitcast(FP8X4),
                lhsT_scale=lhs_q[1][:, lhs_lo : lhs_lo + P],
                rhs=rhs_q[0][:, rhs_lo : rhs_lo + n].bitcast(FP8X4),
                rhs_scale=rhs_q[1][:, rhs_lo : rhs_lo + n],
                start=start,
                stop=stop,
            )

        def x_column(g, tile):
            return PASSES * 2 * P * (tile // 2) + 2 * P * g + P * (tile % 2)

        def by_scalar(dst, src):
            nc.scalar.copy(out=dst, in_=src)

        def by_vector(dst, src):
            nc.vector.tensor_copy(out=dst, in_=src)

        def load_x(b, pieces):
            dst = x_raw[b][:].rearrange("p (u z) -> p u z", u=2)
            src = X[b].rearrange("(u p e) d -> p u (e d)", p=P, e=2)
            n = 2 // pieces
            for k in range(pieces):
                nc.sync.dma_start(out=dst[:, n * k : n * k + n, :], in_=src[:, n * k : n * k + n, :])

        def load_adj(b):
            nc.sync.dma_start(
                out=adj_raw[b][:].rearrange("p (u e) j -> p u (e j)", e=2),
                in_=adj[b].rearrange("(u p e) j -> p u (e j)", p=P, e=2),
            )

        def load_w_e1(c, g):
            for u in range(2):
                rows = W_l1[2 * P * (2 * g + u) : 2 * P * (2 * g + u + 1), BANK * c : BANK * (c + 1)]
                nc.sync.dma_start(out=w_e1_raw[c][g][:, 2 * u : 2 * u + 2, :], in_=rows.rearrange("(p e) c -> p e c", e=2))

        def load_w_out_pass(g):
            dst = w_out_raw[g][:].rearrange("p (u e) c -> p u e c", e=2)
            rows = W_l[P * PACK * g : P * PACK * (g + 1), :]
            nc.sync.dma_start(out=dst, in_=rows.rearrange("(u p e) c -> p u e c", p=P, e=2))

        def warm_up(count, moving=None):
            for i in range(count):
                bank = psum.tile([P, BANK], F32, name="warm_bank", tag="bank")
                rhs = zeros[:] if moving is None else moving
                nc.tensor.matmul(out=bank[:], lhsT=zeros[:, 0:P], rhs=rhs, start=True, stop=True)

        x_grouped = {}

        def transpose_x_half(b, half, copiers):
            if half == 0:
                x_grouped[b] = stage.tile([P, PASSES * NODES * PACK], BF16, name="x_grouped%d" % b, tag="x_grouped", align_bytes=64)
            words = x_raw[b][:].bitcast(F32)
            dst = x_grouped[b][:].bitcast(F32).rearrange("p (h g n u) -> p h g n u", h=2, g=PASSES, u=2)
            banks = []
            for g in range(PASSES):
                bank = psum.tile([P, 2, 2 * P], F32, name="x_bank", tag="bank")
                for u in range(2):
                    for t in range(2):
                        lo = (FEATS // 2) * (2 * half + t) + 2 * P * g + P * u
                        nc.tensor.transpose(bank[:, u, P * t : P * t + P], words[:, lo : lo + P], ident_f32[:])
                banks.append(bank)
            for g in range(PASSES):
                copiers[g](dst[:, half, g, :, :], banks[g][:].rearrange("p u n -> p n u"))

        def transpose_x(b, copiers):
            for half in range(2):
                transpose_x_half(b, half, copiers[2 * half : 2 * half + 2])

        def quantise_x(b):
            quantise(x_q[b], 0, PASSES * NODES, x_grouped[b][:])

        def quantise_x_half(b, half):
            n = PASSES * 2 * P
            quantise(x_q[b], n * half, n, x_grouped[b][:, PACK * n * half : PACK * n * (half + 1)])

        w_grouped = {}

        def regroup_weight(i, g, lo, n, copier):
            tile = stage.tile([P, n, PACK], BF16, name="w_grouped", tag="w_grouped%d" % n, bufs=W_GROUPED_BUFS[n], align_bytes=64)
            w_grouped[(i, g, lo)] = tile
            if i == W_E1:
                raw = w_e1_raw[lo // BANK][g][:, :, lo % BANK : lo % BANK + n]
            else:
                raw = w_out_raw[g][:, :, lo : lo + n]
            copier(tile[:].rearrange("p (c i) t -> p c t i", i=4), raw.rearrange("p t (c i) -> p c t i", i=4))

        def quantise_weight(i, g, lo, n):
            quantise(w_q[i], FEATS * g + lo, n, w_grouped[(i, g, lo)][:].rearrange("p c t -> p (c t)"))

        e1_grouped = {}

        def e1_blocks(b, blocks):
            if b not in e1_grouped:
                e1_grouped[b] = stage.tile([P, FEATS, PACK], BF16, name="e1_grouped%d" % b, tag="e1_grouped", bufs=3, align_bytes=64)
            for block in blocks:
                bank = psum.tile([P, NODE_TILES, P], F32, name="e1_bank", tag="bank")
                for t in range(NODE_TILES):
                    for g in range(PASSES):
                        mx_pass(bank[:, t, :], x_q[b], x_column(g, t), w_q[W_E1], FEATS * g + P * block, P, g == 0, g == PASSES - 1)
                by_scalar(e1_grouped[b][:, P * block : P * block + P, :], bank[:].rearrange("p t c -> p c t"))

        def e1_blocks_wide(b, blocks):
            if b not in e1_grouped:
                e1_grouped[b] = stage.tile([P, FEATS, PACK], BF16, name="e1_grouped%d" % b, tag="e1_grouped", bufs=3, align_bytes=64)
            for block in blocks[::2]:
                lo = P * block
                for half in range(2):
                    bank = psum.tile([P, 2, 2 * P], F32, name="e1_wide_bank", tag="bank")
                    for i in range(2):
                        for g in range(PASSES):
                            mx_pass(bank[:, i, :], x_q[b], x_column(g, 2 * half + i), w_q[W_E1], FEATS * g + lo, 2 * P, g == 0, g == PASSES - 1)
                    by_scalar(e1_grouped[b][:, lo : lo + 2 * P, 2 * half : 2 * half + 2], bank[:].rearrange("p t c -> p c t"))

        def quantise_e1(b, half):
            lo = BANK * half
            quantise(e1_q[b], lo, BANK, e1_grouped[b][:, lo : lo + BANK, :].rearrange("p c t -> p (c t)"))

        adj_n = {}
        adj_grouped = {}

        rowsum = keep.tile([P, GRAPHS, NODE_TILES], F32, name="rowsum")
        r = keep.tile([P, GRAPHS, NODE_TILES], F32, name="r")

        def sum_adj_rows(b):
            for t in range(NODE_TILES):
                unused = stage.tile([P, NODES], BF16, name="unused", tag="unused")
                nc.vector.tensor_scalar(
                    out=unused[:], in0=adj_raw[b][:, t, :], scalar1=1.0, scalar2=None,
                    op0=ALU.mult, op1=ALU.add, accum_out=rowsum[:, b, t : t + 1],
                )

        safe = {}
        inverse = {}

        def both(tile, first):
            return tile[:, first : first + 2, :].rearrange("p b t -> p (b t)")

        def invert_1(first):
            sums = both(rowsum, first)
            safe[first] = stage.tile([P, 2 * NODE_TILES], F32, name="safe", tag="safe")
            nc.vector.scalar_tensor_tensor(out=safe[first][:], in0=sums, scalar=0.0, in1=sums, op0=ALU.is_equal, op1=ALU.add)

        def invert_2(first):
            inverse[first] = stage.tile([P, 2 * NODE_TILES], F32, name="inverse", tag="inverse")
            nc.vector.reciprocal(out=inverse[first][:], in_=safe[first][:])

        def invert_3(first):
            nc.vector.scalar_tensor_tensor(
                out=both(r, first), in0=both(rowsum, first), scalar=0.0, in1=inverse[first][:], op0=ALU.not_equal, op1=ALU.mult
            )

        def scale_adj(b):
            adj_n[b] = stage.tile([P, NODE_TILES, NODES], BF16, name="adj_n%d" % b, tag="adj_n")
            for t in range(NODE_TILES):
                nc.vector.tensor_scalar(
                    out=adj_n[b][:, t, :], in0=adj_raw[b][:, t, :], scalar1=r[:, b, t : t + 1], scalar2=None, op0=ALU.mult
                )

        def transpose_adj(b):
            adj_grouped[b] = stage.tile([P, NODES, PACK], BF16, name="adj_grouped%d" % b, tag="adj_grouped", align_bytes=64)
            words = adj_n[b][:].rearrange("p t j -> p (t j)").bitcast(F32)
            dst = adj_grouped[b][:].rearrange("p r t -> p (r t)").bitcast(F32).rearrange("p (r u) -> p r u", u=2)
            filled = []
            for half in range(2):
                bank = psum.tile([P, 2, 2 * P], F32, name="adj_bank", tag="bank")
                for u in range(2):
                    for row_tile in range(2):
                        lo = (NODES // 2) * (2 * half + row_tile) + P * u
                        nc.tensor.transpose(bank[:, u, P * row_tile : P * row_tile + P], words[:, lo : lo + P], ident_f32[:])
                filled.append(bank)
            for half, bank in enumerate(filled):
                by_scalar(dst[:, 2 * P * half : 2 * P * (half + 1), :], bank[:].rearrange("p u r -> p r u"))

        def quantise_adj(b):
            quantise(adj_q[b], 0, NODES, adj_grouped[b][:].rearrange("p r t -> p (r t)"))

        def leaky_relu(part):
            nc.vector.scalar_tensor_tensor(out=part, in0=part, scalar=SLOPE, in1=part, op0=ALU.mult, op1=ALU.max)

        def store(b, tile, lo, n, part):
            rows = out[b].rearrange("(u p e) d -> u e p d", p=P, e=2)[tile // 2, tile % 2]
            nc.sync.dma_start(out=rows[:, lo : lo + n], in_=part)

        def leaky_relu_and_store(b, tile, lo, n, part):
            leaky_relu(part)
            store(b, tile, lo, n, part)

        def output_part(b, tile, lo, n, part):
            bank = psum.tile([P, BANK], F32, name="out_bank", tag="bank")
            for g in range(PASSES):
                mx_pass(bank[:, 0:n], x_q[b], x_column(g, tile), w_q[W_OUT], FEATS * g + lo, n, g == 0, False)
            mx_pass(bank[:, 0:n], adj_q[b], P * tile, e1_q[b], lo, n, False, True)
            by_scalar(part, bank[:, 0:n])

        results = {}

        def output_tiles(b, tiles):
            for tile in tiles:
                result = stage.tile([P, FEATS], F32, name="result", tag="result", bufs=8)
                for lo in range(0, FEATS, BANK):
                    output_part(b, tile, lo, BANK, result[:, lo : lo + BANK])
                results[(b, tile)] = result

        def output_tiles_half_by_half(b, tiles):
            for tile in tiles:
                result = stage.tile([P, FEATS], F32, name="result", tag="result", bufs=8)
                results[(b, tile)] = result
            for lo in range(0, FEATS, BANK):
                for tile in tiles:
                    output_part(b, tile, lo, BANK, results[(b, tile)][:, lo : lo + BANK])

        def finish_tiles(b, tiles):
            for tile in tiles:
                leaky_relu_and_store(b, tile, 0, FEATS, results[(b, tile)][:])

        def output_tiles_by_halves(b, tiles):
            for tile in tiles:
                result = stage.tile([P, FEATS], F32, name="result", tag="result", bufs=8)
                for lo in range(0, FEATS, BANK):
                    part = result[:, lo : lo + BANK]
                    output_part(b, tile, lo, BANK, part)
                    leaky_relu(part)
                store(b, tile, 0, FEATS, result[:])

        def output_part_tiles(b, tiles, lo, n):
            for tile in tiles:
                result = stage.tile([P, n], F32, name="part_result", tag="result", bufs=8)
                output_part(b, tile, lo, n, result[:])
                leaky_relu_and_store(b, tile, lo, n, result[:])

        load_x(0, 2)
        for g in range(PASSES):
            load_w_e1(0, g)
        load_x(1, 2)
        for g in range(PASSES):
            load_w_e1(1, g)
        load_x(2, 1)
        load_x(3, 1)
        load_adj(0)
        load_adj(1)
        for g in range(PASSES):
            load_w_out_pass(g)
        load_adj(2)
        load_adj(3)

        def regroup_e1_quarter(q, copiers):
            for g in range(PASSES):
                regroup_weight(W_E1, g, quarter * q, quarter, copiers[g])

        def quantise_e1_quarter(q):
            for g in range(PASSES):
                quantise_weight(W_E1, g, quarter * q, quarter)

        def regroup_w_out(g):
            regroup_weight(W_OUT, g, 0, FEATS, by_vector)

        def quantise_w_out(g):
            quantise_weight(W_OUT, g, 0, FEATS)

        def quantise_e1_whole(b):
            quantise(e1_q[b], 0, FEATS, e1_grouped[b][:].rearrange("p c t -> p (c t)"))

        warm_up(5)
        transpose_x_half(0, 0, (by_scalar, by_vector))
        transpose_x_half(0, 1, (by_scalar, by_scalar))
        quantise_x_half(0, 0)
        warm_up(2)
        warm_up(4, w_e1_raw[0][0][:, 0, :])
        regroup_weight(W_E1, 0, 0, quarter, by_vector)
        quantise_x_half(0, 1)
        quantise_weight(W_E1, 0, 0, quarter)
        regroup_weight(W_E1, 0, quarter, quarter, by_scalar)
        regroup_weight(W_E1, 1, 0, quarter, by_vector)
        quantise_weight(W_E1, 0, quarter, quarter)
        quantise_weight(W_E1, 1, 0, quarter)
        warm_up(4, w_e1_raw[0][1][:, 0, :])
        transpose_x_half(1, 0, (by_scalar, by_scalar))
        e1_blocks(0, (0, 1))
        regroup_weight(W_E1, 1, quarter, quarter, by_vector)
        quantise_x_half(1, 0)
        quantise_weight(W_E1, 1, quarter, quarter)
        transpose_x_half(1, 1, (by_scalar, by_vector))
        e1_blocks(0, (2, 3))
        quantise_x_half(1, 1)
        e1_blocks(1, (0, 1))
        regroup_e1_quarter(2, (by_vector, by_vector))
        e1_blocks(1, (2, 3))
        quantise_e1_quarter(2)
        e1_blocks(0, (4, 5))
        regroup_e1_quarter(3, (by_vector, by_vector))
        e1_blocks(1, (4, 5))
        quantise_e1_quarter(3)
        quantise_e1(0, 0)
        quantise_e1(1, 0)
        transpose_x(2, (by_scalar, by_vector, by_scalar, by_scalar))
        sum_adj_rows(0)
        transpose_x(3, (by_scalar,) * 4)
        e1_blocks(0, (6, 7))
        quantise_x(2)
        e1_blocks(1, (6, 7))
        sum_adj_rows(1)
        quantise_x_half(3, 0)
        invert_1(0)
        quantise_x_half(3, 1)
        invert_2(0)
        quantise_e1(0, 1)
        invert_3(0)
        e1_blocks(2, (0, 1, 2, 3))
        scale_adj(0)
        scale_adj(1)
        e1_blocks(2, (4, 5, 6, 7))
        regroup_w_out(0)
        regroup_weight(W_OUT, 1, 0, BANK, by_vector)
        quantise_w_out(0)
        transpose_adj(0)
        transpose_adj(1)
        e1_blocks_wide(3, (0, 1, 2, 3))
        quantise_adj(0)
        quantise_weight(W_OUT, 1, 0, BANK)
        e1_blocks(3, (4, 5, 6, 7))

        regroup_weight(W_OUT, 1, BANK, BANK, by_vector)
        quantise_adj(1)
        quantise_weight(W_OUT, 1, BANK, BANK)
        output_tiles_half_by_half(0, (0, 1, 2, 3))
        sum_adj_rows(2)
        sum_adj_rows(3)
        quantise_e1(1, 1)
        invert_1(2)
        quantise_e1_whole(2)
        invert_2(2)
        finish_tiles(0, (0,))
        invert_3(2)
        finish_tiles(0, (1,))
        scale_adj(2)
        scale_adj(3)
        finish_tiles(0, (2,))
        output_tiles(1, (0,))
        finish_tiles(0, (3,))
        output_tiles(1, (1,))
        transpose_adj(2)
        transpose_adj(3)
        finish_tiles(1, (0,))
        output_tiles(1, (2,))
        quantise_adj(2)
        finish_tiles(1, (1,))
        output_tiles(1, (3,))
        quantise_adj(3)
        finish_tiles(1, (2,))
        finish_tiles(1, (3,))
        quantise_e1_whole(3)
        for tile in range(NODE_TILES):
            output_tiles(2, (tile,))
            finish_tiles(2, (tile,))
        output_tiles_by_halves(3, (0, 1))
        output_part_tiles(3, (2,), 0, BANK)
        output_part_tiles(3, (2,), BANK, BANK)
        output_part_tiles(3, (3,), 0, BANK)
        output_part_tiles(3, (3,), BANK, BANK)
